import numpy as np
import ml_dtypes


def mxq(x, axis, fmt="e4m3"):
    dtype, down = {"e4m3": (ml_dtypes.float8_e4m3fn, 7), "e5m2": (ml_dtypes.float8_e5m2, 14)}[fmt]
    v = np.moveaxis(np.asarray(x, np.float32).astype(ml_dtypes.bfloat16).astype(np.float64), axis, -1)
    blocks = v.reshape(v.shape[:-1] + (-1, 32))
    amax = np.abs(blocks).max(-1, keepdims=True)
    byte = np.maximum(np.where(amax > 0, np.frexp(amax)[1] - 1 + 127, 0) - down, 1)
    scale = np.exp2(byte - 127.0)
    codes = (blocks / scale).astype(np.float32).astype(dtype).astype(np.float64)
    return np.moveaxis((codes * scale).reshape(v.shape), -1, axis)


WIDE = False


def mx_kscale(k):
    if not WIDE:
        return np.ones(k)
    levels = np.array([10, -10, 5, -5, 0])
    if k % 512:
        return np.exp2(np.random.permutation(np.resize(levels, k // 32))).repeat(32)
    a = np.empty((k // 512, 16))
    for p in range(k // 512):
        a[p, :8] = np.random.permutation(np.resize(levels, 8))
        for g in range(8):
            far = levels[np.abs(levels - a[p, g]) >= 10]
            a[p, g + 8] = far[np.random.randint(len(far))]
    return np.exp2(a.ravel()).repeat(32)


BF16 = ml_dtypes.bfloat16


def bf(x):
    return np.asarray(x, np.float32).astype(BF16)


def f64(x):
    return np.asarray(x).astype(np.float64)


S, E, C, HD, HP = 2048, 768, 256, 1024, 1024
R = 2 * HP


def sigmoid(v):
    return 1.0 / (1.0 + np.exp(-v))


def setup_inputs():
    s, t = mx_kscale(R), mx_kscale(HD)
    return {"r": bf(np.abs(np.random.standard_normal((C, R))) * 0.5 * s),
            "psi_w1": bf(np.random.standard_normal((HD, R)) * 2.0 / np.sqrt(R) / s * t[:, None]),
            "psi_b1": bf(np.random.standard_normal(HD) * 0.3 * t),
            "w_dw": bf(np.random.standard_normal((E, HD)) * 1.5 / np.sqrt(HD) / t),
            "b_dw": bf(np.random.standard_normal(E) * 0.3),
            "w_gate": bf(np.random.standard_normal((E, HD)) * 1.5 / np.sqrt(HD) / t),
            "b_gate": bf(np.random.standard_normal(E) * 0.3),
            "W0": bf(np.random.standard_normal(E) * 0.1)}


def reference(r, psi_w1, psi_b1, w_dw, b_dw, w_gate, b_gate, W0):
    hid = np.maximum((mxq(f64(r), 1, "e4m3") @ mxq(f64(psi_w1), 1, "e4m3").T) + f64(psi_b1), 0.0)
    hq = mxq(hid, 1, "e4m3")
    dW = (hq @ mxq(f64(w_dw), 1, "e4m3").T) + f64(b_dw)
    gate = sigmoid((hq @ mxq(f64(w_gate), 1, "e4m3").T) + f64(b_gate))
    return f64(W0)[None, :] + gate * dW

@@ -1,0 +1,345 @@
+from contextlib import ExitStack
+
+import concourse.mybir as mybir
+from concourse.masks import make_identity
+
+F32 = mybir.dt.float32
+BF16 = mybir.dt.bfloat16
+U32 = mybir.dt.uint32
+U8 = mybir.dt.uint8
+FP8X4 = mybir.dt.float8_e4m3fn_x4
+ACT = mybir.ActivationFunctionType
+ALU = mybir.AluOpType
+
+P = 128
+C, R, HD, E = 256, 2048, 1024, 768
+FLOPS = 2 * C * R * HD + 2 * 2 * C * HD * E
+
+PIN = True
+V_BANKS = {0: (1, 3), 1: (3,), 2: (3,), 3: (3,), 4: (3,), 5: (3,), 6: (3,), 7: ()}
+
+
+def tile_metalinearheadml_pb_kernel(tc, r, psi_w1, psi_b1, w_dw, b_dw, w_gate, b_gate, W0, out):
+    nc = tc.nc
+    with ExitStack() as ctx:
+        keep = ctx.enter_context(tc.tile_pool(name="keep", bufs=1))
+        stage = ctx.enter_context(tc.tile_pool(name="stage", bufs=3))
+        ps_pool = ctx.enter_context(tc.psum_pool(name="ps_pool", bufs=8))
+        if PIN:
+            ctx.enter_context(tc.manual_schedule())
+
+        vec_in = keep.tile([P, 512], BF16, name="vec_in")
+        nc.vector.memset(vec_in[:], 0.0)
+        warm = keep.tile([P, 1], F32, name="warm")
+        nc.vector.memset(warm[:], 0.0)
+        warm2 = keep.tile([P, 1], F32, name="warm2")
+        nc.scalar.dma_start(out=vec_in[0:2, :], in_=psi_b1.rearrange("(a w) -> a w", a=2))
+        nc.scalar.dma_start(out=vec_in[4:7, 0:256], in_=b_dw.rearrange("(a w) -> a w", a=3))
+        nc.scalar.dma_start(out=vec_in[7:10, 0:256], in_=b_gate.rearrange("(a w) -> a w", a=3))
+        nc.scalar.dma_start(out=vec_in[10:13, 0:256], in_=W0.rearrange("(a w) -> a w", a=3))
+        nc.scalar.activation(out=warm2[:], in_=warm[:], func=ACT.Sigmoid)
+        ident_f = keep.tile([P, P], F32, name="ident_f")
+        make_identity(nc, ident_f[:])
+        ident_b = keep.tile([P, P], BF16, name="ident_b")
+        make_identity(nc, ident_b[:])
+
+        r_dram = r.rearrange("(a p) k -> p a k", a=2)
+        r_sb = []
+        for h in range(2):
+            t = keep.tile([P, R], BF16, name="r_sb%d" % h)
+            nc.sync.dma_start(out=t[:].rearrange("p (a k) -> p a k", a=2), in_=r_dram[:, :, 1024 * h : 1024 * h + 1024])
+            r_sb.append(t)
+        psi_dram = psi_w1.rearrange("(g p u e) k -> g u e p k", g=2, u=2, e=2)
+        psi_sb = []
+        for a in range(4):
+            t = keep.tile([P, 2 * R], BF16, name="psi_sb%d" % a)
+            for e in range(2):
+                nc.sync.dma_start(out=t[:, R * e : R * e + R], in_=psi_dram[a // 2, a % 2, e])
+            psi_sb.append(t)
+        dw_dram = w_dw.rearrange("(j p e) k -> j p (e k)", j=3, e=2)
+        gt_dram = w_gate.rearrange("(j p e) k -> j p (e k)", j=3, e=2)
+        w_sb = []
+        for j in range(3):
+            tg = keep.tile([P, 2 * HD], BF16, name="gt_sb%d" % j)
+            nc.sync.dma_start(out=tg[:], in_=gt_dram[j])
+            td = keep.tile([P, 2 * HD], BF16, name="dw_sb%d" % j)
+            nc.sync.dma_start(out=td[:], in_=dw_dram[j])
+            w_sb.append((tg, td))
+
+        codes = [keep.tile([P, 1024], U32, name="codes%d" % n, align_bytes=64) for n in range(8)]
+        planes = [keep.tile([P, 1024], U8, name="planes%d" % n, align_bytes=64) for n in range(8)]
+        groups = {}
+        banks = {}
+
+        def slices_of(n, b):
+            if n == 0:
+                src = r_sb[b // 2][:].bitcast(F32)
+                base = 256 * (b % 2)
+                return [src[:, a * 512 + base + u : a * 512 + base + 256 : 2] for u in range(2) for a in range(2)]
+            if n <= 4:
+                src = psi_sb[n - 1][:].bitcast(F32)
+                base = 512 * b
+            else:
+                src = w_sb[n - 5][b // 2][:].bitcast(F32)
+                base = 512 * (b % 2)
+            return [src[:, base + 256 * g + u : base + 256 * g + 256 : 2] for g in range(2) for u in range(2)]
+
+        def transposes(n, bs=(0, 1, 2, 3)):
+            for b in bs:
+                tp = ps_pool.tile([P, 512], F32, name="tp", tag="ps")
+                for i, s in enumerate(slices_of(n, b)):
+                    nc.tensor.transpose(tp[:, 128 * i : 128 * i + 128], s, ident_f[:])
+                banks[(n, b)] = tp
+
+        def empty(n, bs=(0, 1, 2, 3)):
+            if n not in groups:
+                groups[n] = stage.tile([P, 4096], BF16, name="grp", tag="grp", align_bytes=64)
+            gw = groups[n][:].bitcast(F32)
+            for b in bs:
+                tp = banks[(n, b)]
+                dst = gw[:, 512 * b : 512 * b + 512]
+                if n == 0:
+                    o = dst.rearrange("q (c u) -> q c u", u=2)
+                    i = tp[:].rearrange("q (u c) -> q c u", u=2)
+                else:
+                    o = dst.rearrange("q (g m u) -> q g m u", g=2, u=2)
+                    i = tp[:].rearrange("q (g u m) -> q g m u", g=2, u=2)
+                if b in V_BANKS[n]:
+                    nc.vector.tensor_copy(out=o, in_=i)
+                else:
+                    nc.scalar.copy(out=o, in_=i)
+
+        def quantise(n, lo, hi):
+            nc.vector.quantize_mx(
+                out=codes[n][:, 256 * lo : 256 * hi].bitcast(FP8X4),
+                scales=planes[n][:, 256 * lo : 256 * hi],
+                in_=groups[n][:, 1024 * lo : 1024 * hi],
+            )
+
+        vec_w = keep.tile([P, 48], F32, name="vec_w")
+        vec_f = keep.tile([P, 96], F32, name="vec_f")
+        w0_b = keep.tile([P, E], F32, name="w0_b")
+
+        def vec_prep():
+            tpv = ps_pool.tile([P, 512], F32, name="tpv", tag="ps")
+            vw = vec_in[:].bitcast(F32)
+            for i, words in enumerate((vw[:, 0:256:2], vw[:, 1:256:2], vw[:, 0:128])):
+                nc.tensor.transpose(tpv[:, 128 * i : 128 * i + 128], words, ident_f[:])
+            nc.vector.tensor_copy(
+                out=vec_w[:].rearrange("p (i r) -> p i r", i=3),
+                in_=tpv[:, 0:384].rearrange("p (i r) -> p i r", i=3)[:, :, 0:16],
+            )
+            nc.vector.tensor_copy(out=vec_f[:], in_=vec_w[:].bitcast(BF16))
+
+        w0_ps = []
+
+        def w0_mm():
+            vb = vec_w[:].bitcast(BF16)
+            for half, js in ((0, (0, 1)), (1, (2,))):
+                wps = ps_pool.tile([P, 512], F32, name="wps", tag="ps")
+                w0_ps.append(wps)
+                for jj, j in enumerate(js):
+                    for e in range(2):
+                        col = 2 * (32 + 10 + j) + e
+                        nc.tensor.matmul(
+                            wps[:, (jj * 2 + e) * 128 : (jj * 2 + e) * 128 + 128],
+                            lhsT=vb[:, col : col + 1].to_broadcast([P, P]),
+                            rhs=ident_b[:],
+                            start=True,
+                            stop=True,
+                        )
+
+        def w0_out():
+            for half, js in ((0, (0, 1)), (1, (2,))):
+                wps = w0_ps[half]
+                w = 256 * len(js)
+                nc.vector.tensor_copy(
+                    out=w0_b[:, 512 * half : 512 * half + w].rearrange("c (j p e) -> c j p e", p=128, e=2),
+                    in_=wps[:, 0:w].rearrange("c (j e p) -> c j p e", p=128, e=2),
+                )
+
+        hbf = [keep.tile([P, 1024], BF16, name="hbf%d" % g) for g in range(2)]
+        grp_h = [keep.tile([P, 1024], BF16, name="grp_h%d" % g, align_bytes=64) for g in range(2)]
+        codes_h = [keep.tile([P, 256], U32, name="codes_h%d" % g, align_bytes=64) for g in range(2)]
+        planes_h = [keep.tile([P, 256], U8, name="planes_h%d" % g, align_bytes=64) for g in range(2)]
+        accs = {}
+
+        def mm_hidden(n):
+            acc = ps_pool.tile([P, 512], F32, name="acc1", tag="ps")
+            acc_b = acc
+            if n == 4:
+                acc_b = ps_pool.tile([P, 512], F32, name="acc1b", tag="ps")
+            accs[n] = (acc, acc_b)
+            for e in range(2):
+                for g in range(4):
+                    cols = slice((e * 4 + g) * 128, (e * 4 + g) * 128 + 128)
+                    rc = slice(256 * g, 256 * g + 256)
+                    nc.tensor.matmul_mx(
+                        out=accs[n][e][:, 256 * e : 256 * e + 256],
+                        lhsT=codes[n][:, cols].bitcast(FP8X4),
+                        lhsT_scale=planes[n][:, cols],
+                        rhs=codes[0][:, rc].bitcast(FP8X4),
+                        rhs_scale=planes[0][:, rc],
+                        start=(g == 0),
+                        stop=(g == 3),
+                    )
+
+        def relu_hidden(n):
+            a = n - 1
+            g2, u2 = a // 2, a % 2
+            for e in range(2):
+                t = 2 * u2 + e
+                if n == 4 and e == 1:
+                    nc.vector.tensor_scalar(
+                        out=hbf[g2][:, 256 * t : 256 * t + 256],
+                        in0=accs[n][e][:, 256 * e : 256 * e + 256],
+                        scalar1=vec_f[:, 2 * (16 * u2 + g2) + e : 2 * (16 * u2 + g2) + e + 1],
+                        scalar2=0.0,
+                        op0=ALU.add,
+                        op1=ALU.max,
+                    )
+                else:
+                    nc.scalar.activation(
+                        out=hbf[g2][:, 256 * t : 256 * t + 256],
+                        in_=accs[n][e][:, 256 * e : 256 * e + 256],
+                        func=ACT.Relu,
+                        bias=vec_f[:, 2 * (16 * u2 + g2) + e : 2 * (16 * u2 + g2) + e + 1],
+                    )
+
+        def regroup_hidden(g2):
+            nc.vector.tensor_copy(
+                out=grp_h[g2][:].rearrange("p (c i t) -> p c t i", i=4, t=4),
+                in_=hbf[g2][:].rearrange("p (t c i) -> p c t i", t=4, i=4),
+            )
+
+        def quantise_hidden(g2):
+            nc.vector.quantize_mx(out=codes_h[g2][:].bitcast(FP8X4), scales=planes_h[g2][:], in_=grp_h[g2][:])
+
+        out_sb = [keep.tile([P, 512], F32, name="out_sb%d" % j) for j in range(3)]
+        out_dram = out.rearrange("(a c) x -> c a x", a=2)
+        xs = {}
+
+        def mm_out(n, es=(0, 1)):
+            if n not in accs:
+                acc_g = ps_pool.tile([P, 512], F32, name="acc_g", tag="ps")
+                acc_d = ps_pool.tile([P, 512], F32, name="acc_d", tag="ps")
+                accs[n] = (acc_d, acc_g)
+            for mat in (1, 0):
+                for e in es:
+                    for g2 in range(2):
+                        bank = (1 - mat) * 2 + e
+                        cols = slice((bank * 2 + g2) * 128, (bank * 2 + g2) * 128 + 128)
+                        nc.tensor.matmul_mx(
+                            out=accs[n][mat][:, 256 * e : 256 * e + 256],
+                            lhsT=codes[n][:, cols].bitcast(FP8X4),
+                            lhsT_scale=planes[n][:, cols],
+                            rhs=codes_h[g2][:].bitcast(FP8X4),
+                            rhs_scale=planes_h[g2][:],
+                            start=(g2 == 0),
+                            stop=(g2 == 1),
+                        )
+
+        def gate_out(n, es=(0, 1)):
+            j = n - 5
+            if n not in xs:
+                gate = stage.tile([P, 512], F32, name="gate", tag="gate")
+                x = stage.tile([P, 512], F32, name="x", tag="x")
+                xs[n] = (gate, x)
+            gate, x = xs[n]
+            acc_d, acc_g = accs[n]
+            for e in es:
+                cs = slice(256 * e, 256 * e + 256)
+                nc.scalar.activation(
+                    out=gate[:, cs], in_=acc_g[:, cs], func=ACT.Sigmoid, bias=vec_f[:, 2 * (39 + j) + e : 2 * (39 + j) + e + 1]
+                )
+            for e in es:
+                cs = slice(256 * e, 256 * e + 256)
+                nc.vector.scalar_tensor_tensor(
+                    out=x[:, cs],
+                    in0=acc_d[:, cs],
+                    scalar=vec_f[:, 2 * (36 + j) + e : 2 * (36 + j) + e + 1],
+                    in1=gate[:, cs],
+                    op0=ALU.add,
+                    op1=ALU.mult,
+                )
+
+        fins = {}
+
+        def back(n):
+            x = xs[n][1]
+            fin = ps_pool.tile([P, 512], F32, name="fin", tag="ps")
+            for a in range(2):
+                for e in range(2):
+                    nc.tensor.transpose(
+                        fin[:, (a * 2 + e) * 128 : (a * 2 + e) * 128 + 128], x[:, 256 * e + 128 * a : 256 * e + 128 * a + 128], ident_f[:]
+                    )
+            fins[n] = fin
+
+        def finish(n):
+            j = n - 5
+            xc = slice(256 * j, 256 * j + 256)
+            nc.vector.tensor_tensor(
+                out=out_sb[j][:].rearrange("c (a p e) -> c a p e", a=2, e=2),
+                in0=fins[n][:].rearrange("c (a e p) -> c a p e", a=2, e=2),
+                in1=w0_b[:, xc].rearrange("c (p e) -> c p e", e=2).unsqueeze(1).to_broadcast([P, 2, 128, 2]),
+                op=ALU.add,
+            )
+            nc.sync.dma_start(out=out_dram[:, :, xc], in_=out_sb[j][:].rearrange("c (a x) -> c a x", a=2))
+
+        def quantise_all(n):
+            quantise(n, 0, 2)
+            quantise(n, 2, 4)
+
+        transposes(0)
+        empty(0)
+        vec_prep()
+        transposes(1)
+        quantise_all(0)
+        empty(1)
+        w0_mm()
+        transposes(2)
+        quantise_all(1)
+        w0_out()
+        mm_hidden(1)
+        empty(2)
+        transposes(3)
+        quantise_all(2)
+        mm_hidden(2)
+        relu_hidden(1)
+        empty(3)
+        transposes(4)
+        quantise_all(3)
+        mm_hidden(3)
+        relu_hidden(2)
+        regroup_hidden(0)
+        quantise_hidden(0)
+        empty(4)
+        transposes(5)
+        quantise_all(4)
+        mm_hidden(4)
+        relu_hidden(3)
+        empty(5)
+        transposes(6)
+        quantise_all(5)
+        relu_hidden(4)
+        regroup_hidden(1)
+        quantise_hidden(1)
+        empty(6)
+        transposes(7)
+        quantise_all(6)
+        empty(7)
+        mm_out(5)
+        quantise(7, 0, 2)
+        quantise(7, 2, 3)
+        quantise(7, 3, 4)
+        gate_out(5)
+        mm_out(6)
+        gate_out(6)
+        mm_out(7)
+        back(5)
+        back(6)
+        gate_out(7)
+        finish(5)
+        back(7)
+        finish(6)
+        finish(7)

@@ -15,8 +15,8 @@ P = 128
 C, R, HD, E = 256, 2048, 1024, 768
 FLOPS = 2 * C * R * HD + 2 * 2 * C * HD * E
 
-PIN = True
-V_BANKS = {0: (1, 3), 1: (3,), 2: (3,), 3: (3,), 4: (3,), 5: (3,), 6: (3,), 7: ()}
+V_BANKS = {0: (1, 3), 1: (), 2: (), 3: (), 4: (), 5: (), 6: (), 7: (1,)}
+REORDER = {(4, 0): "V", (4, 1): "V", (5, 0): "V", (5, 1): "V", (7, 0): "V", (7, 1): "V"}
 
 
 def tile_metalinearheadml_pb_kernel(tc, r, psi_w1, psi_b1, w_dw, b_dw, w_gate, b_gate, W0, out):
@@ -25,19 +25,14 @@ def tile_metalinearheadml_pb_kernel(tc, r, psi_w1, psi_b1, w_dw, b_dw, w_gate, b
         keep = ctx.enter_context(tc.tile_pool(name="keep", bufs=1))
         stage = ctx.enter_context(tc.tile_pool(name="stage", bufs=3))
         ps_pool = ctx.enter_context(tc.psum_pool(name="ps_pool", bufs=8))
-        if PIN:
-            ctx.enter_context(tc.manual_schedule())
+        ctx.enter_context(tc.manual_schedule())
 
-        vec_in = keep.tile([P, 512], BF16, name="vec_in")
-        nc.vector.memset(vec_in[:], 0.0)
         warm = keep.tile([P, 1], F32, name="warm")
         nc.vector.memset(warm[:], 0.0)
         warm2 = keep.tile([P, 1], F32, name="warm2")
-        nc.scalar.dma_start(out=vec_in[0:2, :], in_=psi_b1.rearrange("(a w) -> a w", a=2))
-        nc.scalar.dma_start(out=vec_in[4:7, 0:256], in_=b_dw.rearrange("(a w) -> a w", a=3))
-        nc.scalar.dma_start(out=vec_in[7:10, 0:256], in_=b_gate.rearrange("(a w) -> a w", a=3))
-        nc.scalar.dma_start(out=vec_in[10:13, 0:256], in_=W0.rearrange("(a w) -> a w", a=3))
         nc.scalar.activation(out=warm2[:], in_=warm[:], func=ACT.Sigmoid)
+        vec_in = keep.tile([P, 512], BF16, name="vec_in")
+        nc.vector.memset(vec_in[:], 0.0)
         ident_f = keep.tile([P, P], F32, name="ident_f")
         make_identity(nc, ident_f[:])
         ident_b = keep.tile([P, P], BF16, name="ident_b")
@@ -45,118 +40,138 @@ def tile_metalinearheadml_pb_kernel(tc, r, psi_w1, psi_b1, w_dw, b_dw, w_gate, b
 
         r_dram = r.rearrange("(a p) k -> p a k", a=2)
         r_sb = []
-        for h in range(2):
-            t = keep.tile([P, R], BF16, name="r_sb%d" % h)
-            nc.sync.dma_start(out=t[:].rearrange("p (a k) -> p a k", a=2), in_=r_dram[:, :, 1024 * h : 1024 * h + 1024])
-            r_sb.append(t)
+        for lo, hi in ((0, 512), (512, 1024), (1024, 2048)):
+            t = keep.tile([P, 2 * (hi - lo)], BF16, name="r_sb%d" % lo)
+            tv = t[:].rearrange("p (a k) -> p a k", a=2)
+            nc.sync.dma_start(out=tv, in_=r_dram[:, :, lo:hi])
+            for k0 in range(0, hi - lo, 512):
+                r_sb.append([t[:].bitcast(F32)[:, (hi - lo) // 2 * a + k0 // 2 : (hi - lo) // 2 * a + k0 // 2 + 256] for a in range(2)])
+        unit_sb = {}
         psi_dram = psi_w1.rearrange("(g p u e) k -> g u e p k", g=2, u=2, e=2)
-        psi_sb = []
-        for a in range(4):
-            t = keep.tile([P, 2 * R], BF16, name="psi_sb%d" % a)
+        for n in range(1, 5):
+            t = keep.tile([P, 2 * R], BF16, name="unit%d" % n)
             for e in range(2):
-                nc.sync.dma_start(out=t[:, R * e : R * e + R], in_=psi_dram[a // 2, a % 2, e])
-            psi_sb.append(t)
-        dw_dram = w_dw.rearrange("(j p e) k -> j p (e k)", j=3, e=2)
-        gt_dram = w_gate.rearrange("(j p e) k -> j p (e k)", j=3, e=2)
-        w_sb = []
+                nc.sync.dma_start(out=t[:, R * e : R * e + R], in_=psi_dram[(n - 1) // 2, (n - 1) % 2, e])
+            unit_sb[n] = t
+            if n == 1:
+                nc.sync.dma_start(out=vec_in[0:2, :], in_=psi_b1.rearrange("(a w) -> a w", a=2))
+                nc.sync.dma_start(out=vec_in[2:8, 0:128], in_=b_dw.rearrange("(a w) -> a w", a=6))
+                nc.sync.dma_start(out=vec_in[8:14, 0:128], in_=b_gate.rearrange("(a w) -> a w", a=6))
+        gt_dram = w_gate.rearrange("(j e p) k -> j p e k", j=3, e=2)
+        dw_dram = w_dw.rearrange("(j e p) k -> j p e k", j=3, e=2)
         for j in range(3):
-            tg = keep.tile([P, 2 * HD], BF16, name="gt_sb%d" % j)
-            nc.sync.dma_start(out=tg[:], in_=gt_dram[j])
-            td = keep.tile([P, 2 * HD], BF16, name="dw_sb%d" % j)
-            nc.sync.dma_start(out=td[:], in_=dw_dram[j])
-            w_sb.append((tg, td))
+            t = keep.tile([P, 2 * R], BF16, name="unit%d" % (5 + j))
+            tv = t[:].rearrange("p (e m k) -> p m e k", e=2, m=2)
+            nc.sync.dma_start(out=tv[:, 0], in_=gt_dram[j])
+            nc.sync.dma_start(out=tv[:, 1], in_=dw_dram[j])
+            unit_sb[5 + j] = t
+        w0_b = keep.tile([P, E], BF16, name="w0_b")
+        nc.sync.dma_start(out=w0_b[:], in_=W0.partition_broadcast(P))
 
         codes = [keep.tile([P, 1024], U32, name="codes%d" % n, align_bytes=64) for n in range(8)]
         planes = [keep.tile([P, 1024], U8, name="planes%d" % n, align_bytes=64) for n in range(8)]
         groups = {}
         banks = {}
+        re_sb = {}
+
+        def reorder(n, h):
+            if (n, h) not in REORDER:
+                return
+            c = slice(1024 * h, 1024 * h + 1024)
+            if n not in re_sb:
+                re_sb[n] = keep.tile([P, 2 * R], BF16, name="re_sb%d" % n)
+            i = unit_sb[n][:].bitcast(F32)[:, c].rearrange("p (g q u) -> p g u q", g=4, u=2)
+            o = re_sb[n][:].bitcast(F32)[:, c].rearrange("p (g u q) -> p g u q", g=4, u=2)
+            if REORDER[(n, h)] == "V":
+                nc.vector.tensor_copy(out=o, in_=i)
+            elif REORDER[(n, h)] == "G":
+                nc.gpsimd.tensor_copy(out=o, in_=i)
+            else:
+                nc.scalar.copy(out=o, in_=i)
 
         def slices_of(n, b):
             if n == 0:
-                src = r_sb[b // 2][:].bitcast(F32)
-                base = 256 * (b % 2)
-                return [src[:, a * 512 + base + u : a * 512 + base + 256 : 2] for u in range(2) for a in range(2)]
-            if n <= 4:
-                src = psi_sb[n - 1][:].bitcast(F32)
-                base = 512 * b
-            else:
-                src = w_sb[n - 5][b // 2][:].bitcast(F32)
-                base = 512 * (b % 2)
+                return [r_sb[b][a][:, u:256:2] for u in range(2) for a in range(2)]
+            if (n, b // 2) in REORDER:
+                src = re_sb[n][:].bitcast(F32)
+                return [src[:, s : s + 128] for s in range(512 * b, 512 * b + 512, 128)]
+            src, base = unit_sb[n][:].bitcast(F32), 512 * b
             return [src[:, base + 256 * g + u : base + 256 * g + 256 : 2] for g in range(2) for u in range(2)]
 
-        def transposes(n, bs=(0, 1, 2, 3)):
-            for b in bs:
-                tp = ps_pool.tile([P, 512], F32, name="tp", tag="ps")
-                for i, s in enumerate(slices_of(n, b)):
-                    nc.tensor.transpose(tp[:, 128 * i : 128 * i + 128], s, ident_f[:])
-                banks[(n, b)] = tp
+        def trb(n, b):
+            tp = ps_pool.tile([P, 512], F32, name="tp", tag="ps")
+            for i, s in enumerate(slices_of(n, b)):
+                nc.tensor.transpose(tp[:, 128 * i : 128 * i + 128], s, ident_f[:])
+            banks[(n, b)] = tp
 
-        def empty(n, bs=(0, 1, 2, 3)):
+        def tr(n, h):
+            trb(n, 2 * h)
+            trb(n, 2 * h + 1)
+
+        def trs(n, b):
+            banks[(n, b)] = []
+            for g in range(2):
+                tp = ps_pool.tile([P, 512], F32, name="tp", tag="ps")
+                for u in range(2):
+                    nc.tensor.transpose(tp[:, 128 * u : 128 * u + 128], slices_of(n, b)[2 * g + u], ident_f[:])
+                banks[(n, b)].append(tp)
+
+        def group(n):
             if n not in groups:
                 groups[n] = stage.tile([P, 4096], BF16, name="grp", tag="grp", align_bytes=64)
-            gw = groups[n][:].bitcast(F32)
-            for b in bs:
-                tp = banks[(n, b)]
-                dst = gw[:, 512 * b : 512 * b + 512]
-                if n == 0:
-                    o = dst.rearrange("q (c u) -> q c u", u=2)
-                    i = tp[:].rearrange("q (u c) -> q c u", u=2)
-                else:
-                    o = dst.rearrange("q (g m u) -> q g m u", g=2, u=2)
-                    i = tp[:].rearrange("q (g u m) -> q g m u", g=2, u=2)
-                if b in V_BANKS[n]:
-                    nc.vector.tensor_copy(out=o, in_=i)
-                else:
-                    nc.scalar.copy(out=o, in_=i)
+            return groups[n][:].bitcast(F32)
 
-        def quantise(n, lo, hi):
+        def ev(n, b):
+            tp = banks[(n, b)]
+            dst = group(n)[:, 512 * b : 512 * b + 512]
+            if n == 0:
+                dst = dst.rearrange("q (c u) -> q c u", u=2)
+                i = tp[:].rearrange("q (u c) -> q c u", u=2)
+            else:
+                dst = dst.rearrange("q (g m u) -> q g m u", g=2, u=2)
+                i = tp[:].rearrange("q (g u m) -> q g m u", g=2, u=2)
+            if b in V_BANKS[n]:
+                nc.vector.tensor_copy(out=dst, in_=i)
+            else:
+                nc.scalar.copy(out=dst, in_=i)
+
+        def evs(n, b):
+            for g in range(2):
+                dst = group(n)[:, 512 * b + 256 * g : 512 * b + 256 * g + 256].rearrange("q (m u) -> q m u", u=2)
+                i = banks[(n, b)][g][:, 0:256].rearrange("q (u m) -> q m u", u=2)
+                if g:
+                    nc.vector.tensor_copy(out=dst, in_=i)
+                else:
+                    nc.scalar.copy(out=dst, in_=i)
+
+        def evh(n, h):
+            ev(n, 2 * h)
+            ev(n, 2 * h + 1)
+
+        def q(n, lo, hi):
             nc.vector.quantize_mx(
                 out=codes[n][:, 256 * lo : 256 * hi].bitcast(FP8X4),
                 scales=planes[n][:, 256 * lo : 256 * hi],
                 in_=groups[n][:, 1024 * lo : 1024 * hi],
             )
 
-        vec_w = keep.tile([P, 48], F32, name="vec_w")
-        vec_f = keep.tile([P, 96], F32, name="vec_f")
-        w0_b = keep.tile([P, E], F32, name="w0_b")
+        def qh(n, h):
+            q(n, 2 * h, 2 * h + 2)
+
+        vec_f = keep.tile([P, 80], F32, name="vec_f")
 
         def vec_prep():
-            tpv = ps_pool.tile([P, 512], F32, name="tpv", tag="ps")
-            vw = vec_in[:].bitcast(F32)
-            for i, words in enumerate((vw[:, 0:256:2], vw[:, 1:256:2], vw[:, 0:128])):
-                nc.tensor.transpose(tpv[:, 128 * i : 128 * i + 128], words, ident_f[:])
+            tpv = ps_pool.tile([P, 1024], BF16, name="tpv", tag="ps")
+            rows = [vec_in[:, t:512:4] for t in range(4)] + [vec_in[:, 0:128]]
+            for i, v in enumerate(rows):
+                nc.tensor.transpose(tpv[:, 128 * i : 128 * i + 128], v, ident_b[:])
             nc.vector.tensor_copy(
-                out=vec_w[:].rearrange("p (i r) -> p i r", i=3),
-                in_=tpv[:, 0:384].rearrange("p (i r) -> p i r", i=3)[:, :, 0:16],
+                out=vec_f[:].rearrange("p (i r) -> p i r", i=5),
+                in_=tpv[:, 0:640].rearrange("p (i r) -> p i r", i=5)[:, :, 0:16],
             )
-            nc.vector.tensor_copy(out=vec_f[:], in_=vec_w[:].bitcast(BF16))
 
-        w0_ps = []
-
-        def w0_mm():
-            vb = vec_w[:].bitcast(BF16)
-            for half, js in ((0, (0, 1)), (1, (2,))):
-                wps = ps_pool.tile([P, 512], F32, name="wps", tag="ps")
-                w0_ps.append(wps)
-                for jj, j in enumerate(js):
-                    for e in range(2):
-                        col = 2 * (32 + 10 + j) + e
-                        nc.tensor.matmul(
-                            wps[:, (jj * 2 + e) * 128 : (jj * 2 + e) * 128 + 128],
-                            lhsT=vb[:, col : col + 1].to_broadcast([P, P]),
-                            rhs=ident_b[:],
-                            start=True,
-                            stop=True,
-                        )
-
-        def w0_out():
-            for half, js in ((0, (0, 1)), (1, (2,))):
-                wps = w0_ps[half]
-                w = 256 * len(js)
-                nc.vector.tensor_copy(
-                    out=w0_b[:, 512 * half : 512 * half + w].rearrange("c (j p e) -> c j p e", p=128, e=2),
-                    in_=wps[:, 0:w].rearrange("c (j e p) -> c j p e", p=128, e=2),
-                )
+        def col(i):
+            return vec_f[:, i : i + 1]
 
         hbf = [keep.tile([P, 1024], BF16, name="hbf%d" % g) for g in range(2)]
         grp_h = [keep.tile([P, 1024], BF16, name="grp_h%d" % g, align_bytes=64) for g in range(2)]
@@ -164,182 +179,218 @@ def tile_metalinearheadml_pb_kernel(tc, r, psi_w1, psi_b1, w_dw, b_dw, w_gate, b
         planes_h = [keep.tile([P, 256], U8, name="planes_h%d" % g, align_bytes=64) for g in range(2)]
         accs = {}
 
-        def mm_hidden(n):
-            acc = ps_pool.tile([P, 512], F32, name="acc1", tag="ps")
-            acc_b = acc
-            if n == 4:
-                acc_b = ps_pool.tile([P, 512], F32, name="acc1b", tag="ps")
-            accs[n] = (acc, acc_b)
-            for e in range(2):
-                for g in range(4):
-                    cols = slice((e * 4 + g) * 128, (e * 4 + g) * 128 + 128)
-                    rc = slice(256 * g, 256 * g + 256)
-                    nc.tensor.matmul_mx(
-                        out=accs[n][e][:, 256 * e : 256 * e + 256],
-                        lhsT=codes[n][:, cols].bitcast(FP8X4),
-                        lhsT_scale=planes[n][:, cols],
-                        rhs=codes[0][:, rc].bitcast(FP8X4),
-                        rhs_scale=planes[0][:, rc],
-                        start=(g == 0),
-                        stop=(g == 3),
-                    )
+        def mmh(n, e):
+            if n not in accs:
+                accs[n] = {}
+            if e == 0 or n == 4:
+                accs[n][e] = ps_pool.tile([P, 512], F32, name="acc1", tag="ps")
+            else:
+                accs[n][e] = accs[n][0]
+            for g in range(4):
+                cols = slice((e * 4 + g) * 128, (e * 4 + g) * 128 + 128)
+                rc = slice(256 * g, 256 * g + 256)
+                nc.tensor.matmul_mx(
+                    out=accs[n][e][:, 256 * e : 256 * e + 256],
+                    lhsT=codes[n][:, cols].bitcast(FP8X4),
+                    lhsT_scale=planes[n][:, cols],
+                    rhs=codes[0][:, rc].bitcast(FP8X4),
+                    rhs_scale=planes[0][:, rc],
+                    start=(g == 0),
+                    stop=(g == 3),
+                )
 
-        def relu_hidden(n):
-            a = n - 1
-            g2, u2 = a // 2, a % 2
-            for e in range(2):
-                t = 2 * u2 + e
-                if n == 4 and e == 1:
-                    nc.vector.tensor_scalar(
-                        out=hbf[g2][:, 256 * t : 256 * t + 256],
-                        in0=accs[n][e][:, 256 * e : 256 * e + 256],
-                        scalar1=vec_f[:, 2 * (16 * u2 + g2) + e : 2 * (16 * u2 + g2) + e + 1],
-                        scalar2=0.0,
-                        op0=ALU.add,
-                        op1=ALU.max,
-                    )
-                else:
-                    nc.scalar.activation(
-                        out=hbf[g2][:, 256 * t : 256 * t + 256],
-                        in_=accs[n][e][:, 256 * e : 256 * e + 256],
-                        func=ACT.Relu,
-                        bias=vec_f[:, 2 * (16 * u2 + g2) + e : 2 * (16 * u2 + g2) + e + 1],
-                    )
+        def relu(n, e, on_vector=False):
+            g2, u2 = (n - 1) // 2, (n - 1) % 2
+            t = 2 * u2 + e
+            dst = hbf[g2][:, 256 * t : 256 * t + 256]
+            src = accs[n][e][:, 256 * e : 256 * e + 256]
+            bias = col(16 * t + g2)
+            if on_vector:
+                nc.vector.tensor_scalar(out=dst, in0=src, scalar1=bias, scalar2=0.0, op0=ALU.add, op1=ALU.max)
+            else:
+                nc.scalar.activation(out=dst, in_=src, func=ACT.Relu, bias=bias)
 
-        def regroup_hidden(g2):
+        def regroup(g2):
             nc.vector.tensor_copy(
                 out=grp_h[g2][:].rearrange("p (c i t) -> p c t i", i=4, t=4),
                 in_=hbf[g2][:].rearrange("p (t c i) -> p c t i", t=4, i=4),
             )
 
-        def quantise_hidden(g2):
+        def quant_hidden(g2):
             nc.vector.quantize_mx(out=codes_h[g2][:].bitcast(FP8X4), scales=planes_h[g2][:], in_=grp_h[g2][:])
 
         out_sb = [keep.tile([P, 512], F32, name="out_sb%d" % j) for j in range(3)]
+        out_sb_e = keep.tile([P, 256], F32, name="out_sb_e")
         out_dram = out.rearrange("(a c) x -> c a x", a=2)
-        xs = {}
+        accg, accd, gates, xs, fins = {}, {}, {}, {}, {}
 
-        def mm_out(n, es=(0, 1)):
-            if n not in accs:
-                acc_g = ps_pool.tile([P, 512], F32, name="acc_g", tag="ps")
-                acc_d = ps_pool.tile([P, 512], F32, name="acc_d", tag="ps")
-                accs[n] = (acc_d, acc_g)
-            for mat in (1, 0):
-                for e in es:
-                    for g2 in range(2):
-                        bank = (1 - mat) * 2 + e
-                        cols = slice((bank * 2 + g2) * 128, (bank * 2 + g2) * 128 + 128)
-                        nc.tensor.matmul_mx(
-                            out=accs[n][mat][:, 256 * e : 256 * e + 256],
-                            lhsT=codes[n][:, cols].bitcast(FP8X4),
-                            lhsT_scale=planes[n][:, cols],
-                            rhs=codes_h[g2][:].bitcast(FP8X4),
-                            rhs_scale=planes_h[g2][:],
-                            start=(g2 == 0),
-                            stop=(g2 == 1),
-                        )
-
-        def gate_out(n, es=(0, 1)):
-            j = n - 5
-            if n not in xs:
-                gate = stage.tile([P, 512], F32, name="gate", tag="gate")
-                x = stage.tile([P, 512], F32, name="x", tag="x")
-                xs[n] = (gate, x)
-            gate, x = xs[n]
-            acc_d, acc_g = accs[n]
-            for e in es:
-                cs = slice(256 * e, 256 * e + 256)
-                nc.scalar.activation(
-                    out=gate[:, cs], in_=acc_g[:, cs], func=ACT.Sigmoid, bias=vec_f[:, 2 * (39 + j) + e : 2 * (39 + j) + e + 1]
-                )
-            for e in es:
-                cs = slice(256 * e, 256 * e + 256)
-                nc.vector.scalar_tensor_tensor(
-                    out=x[:, cs],
-                    in0=acc_d[:, cs],
-                    scalar=vec_f[:, 2 * (36 + j) + e : 2 * (36 + j) + e + 1],
-                    in1=gate[:, cs],
-                    op0=ALU.add,
-                    op1=ALU.mult,
+        def mmo1(n, e, m):
+            store = (accg, accd)[m]
+            if e == 0:
+                store[n] = ps_pool.tile([P, 512], F32, name="acc2", tag="ps")
+            for g2 in range(2):
+                cols = slice(((2 * e + m) * 2 + g2) * 128, ((2 * e + m) * 2 + g2) * 128 + 128)
+                nc.tensor.matmul_mx(
+                    out=store[n][:, 256 * e : 256 * e + 256],
+                    lhsT=codes[n][:, cols].bitcast(FP8X4),
+                    lhsT_scale=planes[n][:, cols],
+                    rhs=codes_h[g2][:].bitcast(FP8X4),
+                    rhs_scale=planes_h[g2][:],
+                    start=(g2 == 0),
+                    stop=(g2 == 1),
                 )
 
-        fins = {}
+        def mmo(n, e):
+            mmo1(n, e, 0)
+            mmo1(n, e, 1)
 
-        def back(n):
-            x = xs[n][1]
-            fin = ps_pool.tile([P, 512], F32, name="fin", tag="ps")
+        def sig(n, e):
+            if e == 0:
+                gates[n] = stage.tile([P, 512], F32, name="gate", tag="gate")
+                xs[n] = stage.tile([P, 512], F32, name="x", tag="x")
+            cs = slice(256 * e, 256 * e + 256)
+            nc.scalar.activation(out=gates[n][:, cs], in_=accg[n][:, cs], func=ACT.Sigmoid, bias=col(72 + 2 * (n - 5) + e))
+
+        def stt(n, e):
+            cs = slice(256 * e, 256 * e + 256)
+            nc.vector.scalar_tensor_tensor(
+                out=xs[n][:, cs], in0=accd[n][:, cs], scalar=col(66 + 2 * (n - 5) + e), in1=gates[n][:, cs], op0=ALU.add, op1=ALU.mult
+            )
+
+        def back(n, e):
+            if e == 0 or n == 7:
+                fins[(n, e)] = ps_pool.tile([P, 512], F32, name="fin", tag="ps")
+            else:
+                fins[(n, e)] = fins[(n, 0)]
             for a in range(2):
-                for e in range(2):
-                    nc.tensor.transpose(
-                        fin[:, (a * 2 + e) * 128 : (a * 2 + e) * 128 + 128], x[:, 256 * e + 128 * a : 256 * e + 128 * a + 128], ident_f[:]
-                    )
-            fins[n] = fin
+                nc.tensor.transpose(
+                    fins[(n, e)][:, 256 * a + 128 * e : 256 * a + 128 * e + 128], xs[n][:, 256 * e + 128 * a : 256 * e + 128 * a + 128], ident_f[:]
+                )
 
-        def finish(n):
+        def fin(n, e=None):
             j = n - 5
-            xc = slice(256 * j, 256 * j + 256)
+            lo, hi = (0, 256) if e is None else (128 * e, 128 * e + 128)
+            xc = slice(256 * j + lo, 256 * j + hi)
+            ov = out_sb[j][:].rearrange("c (a x) -> c a x", a=2)[:, :, lo:hi]
+            if e == 1:
+                ov = out_sb_e[:].rearrange("c (a x) -> c a x", a=2)
+            elif e == 0:
+                ov = out_sb[j][:, 0:256].rearrange("c (a x) -> c a x", a=2)
             nc.vector.tensor_tensor(
-                out=out_sb[j][:].rearrange("c (a p e) -> c a p e", a=2, e=2),
-                in0=fins[n][:].rearrange("c (a e p) -> c a p e", a=2, e=2),
-                in1=w0_b[:, xc].rearrange("c (p e) -> c p e", e=2).unsqueeze(1).to_broadcast([P, 2, 128, 2]),
+                out=ov,
+                in0=fins[(n, 0 if e is None else e)][:].rearrange("c (a x) -> c a x", a=2)[:, :, lo:hi],
+                in1=w0_b[:, xc].unsqueeze(1).to_broadcast([P, 2, hi - lo]),
                 op=ALU.add,
             )
-            nc.sync.dma_start(out=out_dram[:, :, xc], in_=out_sb[j][:].rearrange("c (a x) -> c a x", a=2))
+            nc.sync.dma_start(out=out_dram[:, :, xc], in_=ov)
 
-        def quantise_all(n):
-            quantise(n, 0, 2)
-            quantise(n, 2, 4)
-
-        transposes(0)
-        empty(0)
+        tr(0, 0)
+        tr(0, 1)
+        evh(0, 0)
+        evh(0, 1)
+        tr(1, 0)
+        tr(1, 1)
+        qh(0, 0)
+        qh(0, 1)
         vec_prep()
-        transposes(1)
-        quantise_all(0)
-        empty(1)
-        w0_mm()
-        transposes(2)
-        quantise_all(1)
-        w0_out()
-        mm_hidden(1)
-        empty(2)
-        transposes(3)
-        quantise_all(2)
-        mm_hidden(2)
-        relu_hidden(1)
-        empty(3)
-        transposes(4)
-        quantise_all(3)
-        mm_hidden(3)
-        relu_hidden(2)
-        regroup_hidden(0)
-        quantise_hidden(0)
-        empty(4)
-        transposes(5)
-        quantise_all(4)
-        mm_hidden(4)
-        relu_hidden(3)
-        empty(5)
-        transposes(6)
-        quantise_all(5)
-        relu_hidden(4)
-        regroup_hidden(1)
-        quantise_hidden(1)
-        empty(6)
-        transposes(7)
-        quantise_all(6)
-        empty(7)
-        mm_out(5)
-        quantise(7, 0, 2)
-        quantise(7, 2, 3)
-        quantise(7, 3, 4)
-        gate_out(5)
-        mm_out(6)
-        gate_out(6)
-        mm_out(7)
-        back(5)
-        back(6)
-        gate_out(7)
-        finish(5)
-        back(7)
-        finish(6)
-        finish(7)
+        evh(1, 0)
+        evh(1, 1)
+        tr(2, 0)
+        tr(2, 1)
+        qh(1, 0)
+        qh(1, 1)
+        evh(2, 0)
+        evh(2, 1)
+        tr(3, 0)
+        mmh(1, 0)
+        mmh(1, 1)
+        tr(3, 1)
+        qh(2, 0)
+        qh(2, 1)
+        evh(3, 0)
+        evh(3, 1)
+        relu(1, 0)
+        relu(1, 1)
+        mmh(2, 0)
+        mmh(2, 1)
+        reorder(4, 0)
+        reorder(4, 1)
+        tr(4, 0)
+        tr(4, 1)
+        qh(3, 0)
+        qh(3, 1)
+        mmh(3, 0)
+        mmh(3, 1)
+        relu(2, 0)
+        relu(2, 1)
+        reorder(5, 0)
+        reorder(5, 1)
+        evh(4, 0)
+        evh(4, 1)
+        tr(5, 0)
+        tr(5, 1)
+        regroup(0)
+        qh(4, 0)
+        quant_hidden(0)
+        qh(4, 1)
+        mmh(4, 0)
+        mmh(4, 1)
+        relu(3, 0)
+        relu(3, 1)
+        reorder(6, 0)
+        reorder(6, 1)
+        evh(5, 0)
+        evh(5, 1)
+        tr(6, 0)
+        tr(6, 1)
+        reorder(7, 0)
+        reorder(7, 1)
+        relu(4, 0)
+        relu(4, 1, True)
+        qh(5, 0)
+        regroup(1)
+        qh(5, 1)
+        quant_hidden(1)
+        evh(6, 0)
+        evh(6, 1)
+        tr(7, 0)
+        mmo(5, 0)
+        mmo(5, 1)
+        trb(7, 2)
+        trs(7, 3)
+        qh(6, 0)
+        qh(6, 1)
+        ev(7, 0)
+        ev(7, 1)
+        sig(5, 0)
+        sig(5, 1)
+        ev(7, 2)
+        evs(7, 3)
+        qh(7, 0)
+        stt(5, 0)
+        stt(5, 1)
+        mmo(6, 0)
+        mmo(6, 1)
+        sig(6, 0)
+        sig(6, 1)
+        q(7, 2, 3)
+        q(7, 3, 4)
+        mmo(7, 0)
+        mmo1(7, 1, 0)
+        mmo1(7, 1, 1)
+        stt(6, 0)
+        stt(6, 1)
+        back(5, 0)
+        back(5, 1)
+        sig(7, 0)
+        stt(7, 0)
+        fin(5)
+        back(6, 0)
+        back(6, 1)
+        sig(7, 1)
+        stt(7, 1)
+        fin(6)
+        back(7, 0)
+        back(7, 1)
+        fin(7, 0)
+        fin(7, 1)

@@ -33,6 +33,9 @@ def tile_metalinearheadml_pb_kernel(tc, r, psi_w1, psi_b1, w_dw, b_dw, w_gate, b
         nc.scalar.activation(out=warm2[:], in_=warm[:], func=ACT.Sigmoid)
         vec_in = keep.tile([P, 512], BF16, name="vec_in")
         nc.vector.memset(vec_in[:], 0.0)
+        nc.scalar.dma_start(out=vec_in[0:2, :], in_=psi_b1.rearrange("(a w) -> a w", a=2))
+        nc.scalar.dma_start(out=vec_in[2:4, 0:384], in_=b_dw.rearrange("(a w) -> a w", a=2))
+        nc.scalar.dma_start(out=vec_in[4:6, 0:384], in_=b_gate.rearrange("(a w) -> a w", a=2))
         ident_f = keep.tile([P, P], F32, name="ident_f")
         make_identity(nc, ident_f[:])
         ident_b = keep.tile([P, P], BF16, name="ident_b")
@@ -53,10 +56,6 @@ def tile_metalinearheadml_pb_kernel(tc, r, psi_w1, psi_b1, w_dw, b_dw, w_gate, b
             for e in range(2):
                 nc.sync.dma_start(out=t[:, R * e : R * e + R], in_=psi_dram[(n - 1) // 2, (n - 1) % 2, e])
             unit_sb[n] = t
-            if n == 1:
-                nc.sync.dma_start(out=vec_in[0:2, :], in_=psi_b1.rearrange("(a w) -> a w", a=2))
-                nc.sync.dma_start(out=vec_in[2:8, 0:128], in_=b_dw.rearrange("(a w) -> a w", a=6))
-                nc.sync.dma_start(out=vec_in[8:14, 0:128], in_=b_gate.rearrange("(a w) -> a w", a=6))
         gt_dram = w_gate.rearrange("(j e p) k -> j p e k", j=3, e=2)
         dw_dram = w_dw.rearrange("(j e p) k -> j p e k", j=3, e=2)
         for j in range(3):
@@ -158,20 +157,24 @@ def tile_metalinearheadml_pb_kernel(tc, r, psi_w1, psi_b1, w_dw, b_dw, w_gate, b
         def qh(n, h):
             q(n, 2 * h, 2 * h + 2)
 
-        vec_f = keep.tile([P, 80], F32, name="vec_f")
+        vec_f = keep.tile([P, 56], F32, name="vec_f")
 
         def vec_prep():
             tpv = ps_pool.tile([P, 1024], BF16, name="tpv", tag="ps")
-            rows = [vec_in[:, t:512:4] for t in range(4)] + [vec_in[:, 0:128]]
+            rows = [vec_in[:, t:512:4] for t in range(4)] + [vec_in[:, s : s + 128] for s in range(0, 384, 128)]
             for i, v in enumerate(rows):
                 nc.tensor.transpose(tpv[:, 128 * i : 128 * i + 128], v, ident_b[:])
             nc.vector.tensor_copy(
-                out=vec_f[:].rearrange("p (i r) -> p i r", i=5),
-                in_=tpv[:, 0:640].rearrange("p (i r) -> p i r", i=5)[:, :, 0:16],
+                out=vec_f[:].rearrange("p (i r) -> p i r", i=7),
+                in_=tpv[:, 0:896].rearrange("p (i r) -> p i r", i=7)[:, :, 0:8],
             )
 
         def col(i):
             return vec_f[:, i : i + 1]
+
+        def col_w(row, n, e):
+            blk = 2 * (n - 5) + e
+            return col(8 * (4 + blk % 3) + row + blk // 3)
 
         hbf = [keep.tile([P, 1024], BF16, name="hbf%d" % g) for g in range(2)]
         grp_h = [keep.tile([P, 1024], BF16, name="grp_h%d" % g, align_bytes=64) for g in range(2)]
@@ -204,7 +207,7 @@ def tile_metalinearheadml_pb_kernel(tc, r, psi_w1, psi_b1, w_dw, b_dw, w_gate, b
             t = 2 * u2 + e
             dst = hbf[g2][:, 256 * t : 256 * t + 256]
             src = accs[n][e][:, 256 * e : 256 * e + 256]
-            bias = col(16 * t + g2)
+            bias = col(8 * t + g2)
             if on_vector:
                 nc.vector.tensor_scalar(out=dst, in0=src, scalar1=bias, scalar2=0.0, op0=ALU.add, op1=ALU.max)
             else:
@@ -249,12 +252,12 @@ def tile_metalinearheadml_pb_kernel(tc, r, psi_w1, psi_b1, w_dw, b_dw, w_gate, b
                 gates[n] = stage.tile([P, 512], F32, name="gate", tag="gate")
                 xs[n] = stage.tile([P, 512], F32, name="x", tag="x")
             cs = slice(256 * e, 256 * e + 256)
-            nc.scalar.activation(out=gates[n][:, cs], in_=accg[n][:, cs], func=ACT.Sigmoid, bias=col(72 + 2 * (n - 5) + e))
+            nc.scalar.activation(out=gates[n][:, cs], in_=accg[n][:, cs], func=ACT.Sigmoid, bias=col_w(4, n, e))
 
         def stt(n, e):
             cs = slice(256 * e, 256 * e + 256)
             nc.vector.scalar_tensor_tensor(
-                out=xs[n][:, cs], in0=accd[n][:, cs], scalar=col(66 + 2 * (n - 5) + e), in1=gates[n][:, cs], op0=ALU.add, op1=ALU.mult
+                out=xs[n][:, cs], in0=accd[n][:, cs], scalar=col_w(2, n, e), in1=gates[n][:, cs], op0=ALU.add, op1=ALU.mult
             )
 
         def back(n, e):

@@ -15,8 +15,8 @@ P = 128
 C, R, HD, E = 256, 2048, 1024, 768
 FLOPS = 2 * C * R * HD + 2 * 2 * C * HD * E
 
-V_BANKS = {0: (1, 3), 1: (), 2: (), 3: (), 4: (), 5: (), 6: (), 7: (1,)}
-REORDER = {(4, 0): "V", (4, 1): "V", (5, 0): "V", (5, 1): "V", (7, 0): "V", (7, 1): "V"}
+V_BANKS = {0: (1, 3), 1: (3,), 2: (3,), 3: (3,), 4: (3,), 5: (3,), 6: (3,), 7: (1, )}
+REORDER = {}
 
 
 def tile_metalinearheadml_pb_kernel(tc, r, psi_w1, psi_b1, w_dw, b_dw, w_gate, b_gate, W0, out):

@@ -15,8 +15,9 @@ P = 128
 C, R, HD, E = 256, 2048, 1024, 768
 FLOPS = 2 * C * R * HD + 2 * 2 * C * HD * E
 
-V_BANKS = {0: (1, 3), 1: (3,), 2: (3,), 3: (3,), 4: (3,), 5: (3,), 6: (3,), 7: (1, )}
-REORDER = {}
+V_BANKS = {0: (1, 3), 1: (3,), 2: (3,), 3: (3,), 4: (), 5: (), 6: (), 7: (1,)}
+BY_K = (1, 2)
+REORDER = {(5, 0): "V", (5, 1): "V", (6, 0): "V", (6, 1): "V", (7, 0): "V", (7, 1): "V"}
 
 
 def tile_metalinearheadml_pb_kernel(tc, r, psi_w1, psi_b1, w_dw, b_dw, w_gate, b_gate, W0, out):
@@ -31,31 +32,48 @@ def tile_metalinearheadml_pb_kernel(tc, r, psi_w1, psi_b1, w_dw, b_dw, w_gate, b
         nc.vector.memset(warm[:], 0.0)
         warm2 = keep.tile([P, 1], F32, name="warm2")
         nc.scalar.activation(out=warm2[:], in_=warm[:], func=ACT.Sigmoid)
-        vec_in = keep.tile([P, 512], BF16, name="vec_in")
+        vec_in = keep.tile([P, 384], BF16, name="vec_in")
         nc.vector.memset(vec_in[:], 0.0)
-        nc.scalar.dma_start(out=vec_in[0:2, :], in_=psi_b1.rearrange("(a w) -> a w", a=2))
-        nc.scalar.dma_start(out=vec_in[2:4, 0:384], in_=b_dw.rearrange("(a w) -> a w", a=2))
-        nc.scalar.dma_start(out=vec_in[4:6, 0:384], in_=b_gate.rearrange("(a w) -> a w", a=2))
+        for g in range(2):
+            nc.scalar.dma_start(
+                out=vec_in[2 * g : 2 * g + 2, 0:256].rearrange("u (b x) -> u b x", x=4),
+                in_=psi_b1[512 * g : 512 * g + 512].rearrange("(b u x) -> u b x", u=2, x=4),
+            )
+        nc.scalar.dma_start(out=vec_in[4:6, 0:384], in_=b_dw.rearrange("(a w) -> a w", a=2))
+        nc.scalar.dma_start(out=vec_in[6:8, 0:384], in_=b_gate.rearrange("(a w) -> a w", a=2))
         ident_f = keep.tile([P, P], F32, name="ident_f")
         make_identity(nc, ident_f[:])
+        perm_f = keep.tile([P, P], F32, name="perm_f")
+        nc.gpsimd.tensor_copy(
+            out=perm_f[:].rearrange("p (v b) -> p v b", v=2), in_=ident_f[:].rearrange("p (b v) -> p v b", v=2)
+        )
         ident_b = keep.tile([P, P], BF16, name="ident_b")
         make_identity(nc, ident_b[:])
 
         r_dram = r.rearrange("(a p) k -> p a k", a=2)
         r_sb = []
-        for lo, hi in ((0, 512), (512, 1024), (1024, 2048)):
-            t = keep.tile([P, 2 * (hi - lo)], BF16, name="r_sb%d" % lo)
-            tv = t[:].rearrange("p (a k) -> p a k", a=2)
-            nc.sync.dma_start(out=tv, in_=r_dram[:, :, lo:hi])
-            for k0 in range(0, hi - lo, 512):
-                r_sb.append([t[:].bitcast(F32)[:, (hi - lo) // 2 * a + k0 // 2 : (hi - lo) // 2 * a + k0 // 2 + 256] for a in range(2)])
+        for h in range(2):
+            t = keep.tile([P, R], BF16, name="r_sb%d" % h)
+            nc.sync.dma_start(out=t[:].rearrange("p (a k) -> p a k", a=2), in_=r_dram[:, :, 1024 * h : 1024 * h + 1024])
+            for b in range(2):
+                r_sb.append([t[:].bitcast(F32)[:, 512 * a + 256 * b : 512 * a + 256 * b + 256] for a in range(2)])
         unit_sb = {}
-        psi_dram = psi_w1.rearrange("(g p u e) k -> g u e p k", g=2, u=2, e=2)
+        psi_dram = psi_w1.rearrange("(g p i e) k -> g e p i k", g=2, i=2, e=2)
+        psi_sb = {}
         for n in range(1, 5):
+            src = psi_dram[(n - 1) // 2, (n - 1) % 2]
             t = keep.tile([P, 2 * R], BF16, name="unit%d" % n)
-            for e in range(2):
-                nc.sync.dma_start(out=t[:, R * e : R * e + R], in_=psi_dram[(n - 1) // 2, (n - 1) % 2, e])
-            unit_sb[n] = t
+            for h in range(2):
+                if n in BY_K:
+                    half = t[:, R * h : R * h + R].rearrange("p (i k) -> p i k", i=2)
+                    nc.sync.dma_start(out=half, in_=src[:, :, 1024 * h : 1024 * h + 1024])
+                    for b in range(2):
+                        psi_sb[(n, 2 * h + b)] = [t[:].bitcast(F32)[:, 1024 * h + 512 * i + 256 * b : 1024 * h + 512 * i + 256 * b + 256] for i in range(2)]
+                else:
+                    nc.sync.dma_start(out=t[:, R * h : R * h + R], in_=src[:, h])
+            if n not in BY_K:
+                for b in range(4):
+                    psi_sb[(n, b)] = [t[:].bitcast(F32)[:, 1024 * i + 256 * b : 1024 * i + 256 * b + 256] for i in range(2)]
         gt_dram = w_gate.rearrange("(j e p) k -> j p e k", j=3, e=2)
         dw_dram = w_dw.rearrange("(j e p) k -> j p e k", j=3, e=2)
         for j in range(3):
@@ -76,31 +94,28 @@ def tile_metalinearheadml_pb_kernel(tc, r, psi_w1, psi_b1, w_dw, b_dw, w_gate, b
         def reorder(n, h):
             if (n, h) not in REORDER:
                 return
-            c = slice(1024 * h, 1024 * h + 1024)
             if n not in re_sb:
-                re_sb[n] = keep.tile([P, 2 * R], BF16, name="re_sb%d" % n)
-            i = unit_sb[n][:].bitcast(F32)[:, c].rearrange("p (g q u) -> p g u q", g=4, u=2)
-            o = re_sb[n][:].bitcast(F32)[:, c].rearrange("p (g u q) -> p g u q", g=4, u=2)
-            if REORDER[(n, h)] == "V":
+                re_sb[n] = keep.tile([P, 4096], BF16, name="re_sb%d" % n)
+            i = unit_sb[n][:, 2048 * h : 2048 * h + 2048].rearrange("p (b u x) -> p u b x", u=2, x=4)
+            o = re_sb[n][:, 2048 * h : 2048 * h + 2048].rearrange("p (u b x) -> p u b x", u=2, x=4)
+            if REORDER.get((n, h), "V") == "V":
                 nc.vector.tensor_copy(out=o, in_=i)
-            elif REORDER[(n, h)] == "G":
-                nc.gpsimd.tensor_copy(out=o, in_=i)
             else:
                 nc.scalar.copy(out=o, in_=i)
 
         def slices_of(n, b):
             if n == 0:
                 return [r_sb[b][a][:, u:256:2] for u in range(2) for a in range(2)]
-            if (n, b // 2) in REORDER:
-                src = re_sb[n][:].bitcast(F32)
-                return [src[:, s : s + 128] for s in range(512 * b, 512 * b + 512, 128)]
-            src, base = unit_sb[n][:].bitcast(F32), 512 * b
-            return [src[:, base + 256 * g + u : base + 256 * g + 256 : 2] for g in range(2) for u in range(2)]
+            if n < 5:
+                return [psi_sb[(n, b)][i][:, u:256:2] for i in range(2) for u in range(2)]
+            src = re_sb[n][:].bitcast(F32)
+            starts = [1024 * (b // 2) + 512 * u + 256 * (b % 2) + 128 * g for g in range(2) for u in range(2)]
+            return [src[:, s : s + 128] for s in starts]
 
         def trb(n, b):
             tp = ps_pool.tile([P, 512], F32, name="tp", tag="ps")
             for i, s in enumerate(slices_of(n, b)):
-                nc.tensor.transpose(tp[:, 128 * i : 128 * i + 128], s, ident_f[:])
+                nc.tensor.transpose(tp[:, 128 * i : 128 * i + 128], s, perm_f[:] if 1 <= n <= 4 else ident_f[:])
             banks[(n, b)] = tp
 
         def tr(n, h):
@@ -126,6 +141,9 @@ def tile_metalinearheadml_pb_kernel(tc, r, psi_w1, psi_b1, w_dw, b_dw, w_gate, b
             if n == 0:
                 dst = dst.rearrange("q (c u) -> q c u", u=2)
                 i = tp[:].rearrange("q (u c) -> q c u", u=2)
+            elif n < 5:
+                dst = dst.rearrange("q (v b x) -> q v b x", v=2, x=4)
+                i = tp[:].rearrange("q (x v b) -> q v b x", x=4, v=2)
             else:
                 dst = dst.rearrange("q (g m u) -> q g m u", g=2, u=2)
                 i = tp[:].rearrange("q (g u m) -> q g m u", g=2, u=2)
@@ -157,16 +175,16 @@ def tile_metalinearheadml_pb_kernel(tc, r, psi_w1, psi_b1, w_dw, b_dw, w_gate, b
         def qh(n, h):
             q(n, 2 * h, 2 * h + 2)
 
-        vec_f = keep.tile([P, 56], F32, name="vec_f")
+        vec_f = keep.tile([P, 40], F32, name="vec_f")
 
         def vec_prep():
             tpv = ps_pool.tile([P, 1024], BF16, name="tpv", tag="ps")
-            rows = [vec_in[:, t:512:4] for t in range(4)] + [vec_in[:, s : s + 128] for s in range(0, 384, 128)]
+            rows = [vec_in[:, e:256:2] for e in range(2)] + [vec_in[:, s : s + 128] for s in range(0, 384, 128)]
             for i, v in enumerate(rows):
                 nc.tensor.transpose(tpv[:, 128 * i : 128 * i + 128], v, ident_b[:])
             nc.vector.tensor_copy(
-                out=vec_f[:].rearrange("p (i r) -> p i r", i=7),
-                in_=tpv[:, 0:896].rearrange("p (i r) -> p i r", i=7)[:, :, 0:8],
+                out=vec_f[:].rearrange("p (i r) -> p i r", i=5),
+                in_=tpv[:, 0:640].rearrange("p (i r) -> p i r", i=5)[:, :, 0:8],
             )
 
         def col(i):
@@ -174,7 +192,7 @@ def tile_metalinearheadml_pb_kernel(tc, r, psi_w1, psi_b1, w_dw, b_dw, w_gate, b
 
         def col_w(row, n, e):
             blk = 2 * (n - 5) + e
-            return col(8 * (4 + blk % 3) + row + blk // 3)
+            return col(8 * (2 + blk % 3) + row + blk // 3)
 
         hbf = [keep.tile([P, 1024], BF16, name="hbf%d" % g) for g in range(2)]
         grp_h = [keep.tile([P, 1024], BF16, name="grp_h%d" % g, align_bytes=64) for g in range(2)]
@@ -190,7 +208,7 @@ def tile_metalinearheadml_pb_kernel(tc, r, psi_w1, psi_b1, w_dw, b_dw, w_gate, b
             else:
                 accs[n][e] = accs[n][0]
             for g in range(4):
-                cols = slice((e * 4 + g) * 128, (e * 4 + g) * 128 + 128)
+                cols = slice((2 * g + e) * 128, (2 * g + e) * 128 + 128)
                 rc = slice(256 * g, 256 * g + 256)
                 nc.tensor.matmul_mx(
                     out=accs[n][e][:, 256 * e : 256 * e + 256],
@@ -202,12 +220,12 @@ def tile_metalinearheadml_pb_kernel(tc, r, psi_w1, psi_b1, w_dw, b_dw, w_gate, b
                     stop=(g == 3),
                 )
 
-        def relu(n, e, on_vector=False):
-            g2, u2 = (n - 1) // 2, (n - 1) % 2
-            t = 2 * u2 + e
+        def relu(n, u, on_vector=False):
+            g2, e = (n - 1) // 2, (n - 1) % 2
+            t = 2 * u + e
             dst = hbf[g2][:, 256 * t : 256 * t + 256]
-            src = accs[n][e][:, 256 * e : 256 * e + 256]
-            bias = col(8 * t + g2)
+            src = accs[n][u][:, 256 * u : 256 * u + 256]
+            bias = col(8 * e + 2 * g2 + u)
             if on_vector:
                 nc.vector.tensor_scalar(out=dst, in0=src, scalar1=bias, scalar2=0.0, op0=ALU.add, op1=ALU.max)
             else:
@@ -252,12 +270,12 @@ def tile_metalinearheadml_pb_kernel(tc, r, psi_w1, psi_b1, w_dw, b_dw, w_gate, b
                 gates[n] = stage.tile([P, 512], F32, name="gate", tag="gate")
                 xs[n] = stage.tile([P, 512], F32, name="x", tag="x")
             cs = slice(256 * e, 256 * e + 256)
-            nc.scalar.activation(out=gates[n][:, cs], in_=accg[n][:, cs], func=ACT.Sigmoid, bias=col_w(4, n, e))
+            nc.scalar.activation(out=gates[n][:, cs], in_=accg[n][:, cs], func=ACT.Sigmoid, bias=col_w(6, n, e))
 
         def stt(n, e):
             cs = slice(256 * e, 256 * e + 256)
             nc.vector.scalar_tensor_tensor(
-                out=xs[n][:, cs], in0=accd[n][:, cs], scalar=col_w(2, n, e), in1=gates[n][:, cs], op0=ALU.add, op1=ALU.mult
+                out=xs[n][:, cs], in0=accd[n][:, cs], scalar=col_w(4, n, e), in1=gates[n][:, cs], op0=ALU.add, op1=ALU.mult
             )
 
         def back(n, e):

@@ -15,7 +15,7 @@ P = 128
 C, R, HD, E = 256, 2048, 1024, 768
 FLOPS = 2 * C * R * HD + 2 * 2 * C * HD * E
 
-V_BANKS = {0: (1, 3), 1: (3,), 2: (3,), 3: (3,), 4: (), 5: (), 6: (), 7: (1,)}
+V_BANKS = {0: (1, 3), 1: (3,), 2: (3,), 3: (3,), 4: (), 5: (), 6: (), 7: ()}
 BY_K = (1, 2)
 REORDER = {(5, 0): "V", (5, 1): "V", (6, 0): "V", (6, 1): "V", (7, 0): "V", (7, 1): "V"}
 
@@ -32,15 +32,12 @@ def tile_metalinearheadml_pb_kernel(tc, r, psi_w1, psi_b1, w_dw, b_dw, w_gate, b
         nc.vector.memset(warm[:], 0.0)
         warm2 = keep.tile([P, 1], F32, name="warm2")
         nc.scalar.activation(out=warm2[:], in_=warm[:], func=ACT.Sigmoid)
-        vec_in = keep.tile([P, 384], BF16, name="vec_in")
+        vec_in = keep.tile([P, E], BF16, name="vec_in")
         nc.vector.memset(vec_in[:], 0.0)
-        for g in range(2):
-            nc.scalar.dma_start(
-                out=vec_in[2 * g : 2 * g + 2, 0:256].rearrange("u (b x) -> u b x", x=4),
-                in_=psi_b1[512 * g : 512 * g + 512].rearrange("(b u x) -> u b x", u=2, x=4),
-            )
-        nc.scalar.dma_start(out=vec_in[4:6, 0:384], in_=b_dw.rearrange("(a w) -> a w", a=2))
-        nc.scalar.dma_start(out=vec_in[6:8, 0:384], in_=b_gate.rearrange("(a w) -> a w", a=2))
+        b1_raw = keep.tile([2, 512], BF16, name="b1_raw")
+        nc.scalar.dma_start(out=b1_raw[:], in_=psi_b1.rearrange("(a w) -> a w", a=2))
+        nc.scalar.dma_start(out=vec_in[2:3, :], in_=b_dw.rearrange("(o w) -> o w", o=1))
+        nc.scalar.dma_start(out=vec_in[3:4, :], in_=b_gate.rearrange("(o w) -> o w", o=1))
         ident_f = keep.tile([P, P], F32, name="ident_f")
         make_identity(nc, ident_f[:])
         perm_f = keep.tile([P, P], F32, name="perm_f")
@@ -74,13 +71,12 @@ def tile_metalinearheadml_pb_kernel(tc, r, psi_w1, psi_b1, w_dw, b_dw, w_gate, b
             if n not in BY_K:
                 for b in range(4):
                     psi_sb[(n, b)] = [t[:].bitcast(F32)[:, 1024 * i + 256 * b : 1024 * i + 256 * b + 256] for i in range(2)]
-        gt_dram = w_gate.rearrange("(j e p) k -> j p e k", j=3, e=2)
-        dw_dram = w_dw.rearrange("(j e p) k -> j p e k", j=3, e=2)
+        gt_dram = w_gate.rearrange("(j p e) k -> j p (e k)", j=3, e=2)
+        dw_dram = w_dw.rearrange("(j p e) k -> j p (e k)", j=3, e=2)
         for j in range(3):
             t = keep.tile([P, 2 * R], BF16, name="unit%d" % (5 + j))
-            tv = t[:].rearrange("p (e m k) -> p m e k", e=2, m=2)
-            nc.sync.dma_start(out=tv[:, 0], in_=gt_dram[j])
-            nc.sync.dma_start(out=tv[:, 1], in_=dw_dram[j])
+            nc.sync.dma_start(out=t[:, 0:R], in_=gt_dram[j])
+            nc.sync.dma_start(out=t[:, R : 2 * R], in_=dw_dram[j])
             unit_sb[5 + j] = t
         w0_b = keep.tile([P, E], BF16, name="w0_b")
         nc.sync.dma_start(out=w0_b[:], in_=W0.partition_broadcast(P))
@@ -109,7 +105,7 @@ def tile_metalinearheadml_pb_kernel(tc, r, psi_w1, psi_b1, w_dw, b_dw, w_gate, b
             if n < 5:
                 return [psi_sb[(n, b)][i][:, u:256:2] for i in range(2) for u in range(2)]
             src = re_sb[n][:].bitcast(F32)
-            starts = [1024 * (b // 2) + 512 * u + 256 * (b % 2) + 128 * g for g in range(2) for u in range(2)]
+            starts = [1024 * (b % 2) + 512 * u + 256 * (b // 2) + 128 * g for g in range(2) for u in range(2)]
             return [src[:, s : s + 128] for s in starts]
 
         def trb(n, b):
@@ -175,24 +171,27 @@ def tile_metalinearheadml_pb_kernel(tc, r, psi_w1, psi_b1, w_dw, b_dw, w_gate, b
         def qh(n, h):
             q(n, 2 * h, 2 * h + 2)
 
-        vec_f = keep.tile([P, 40], F32, name="vec_f")
+        vec_f = keep.tile([P, 48], F32, name="vec_f")
+
+        def vec_order():
+            nc.vector.tensor_copy(
+                out=vec_in[0:2, 0:512].rearrange("p (u b x) -> p u b x", u=2, x=4),
+                in_=b1_raw[:].rearrange("p (b u x) -> p u b x", u=2, x=4),
+            )
 
         def vec_prep():
             tpv = ps_pool.tile([P, 1024], BF16, name="tpv", tag="ps")
-            rows = [vec_in[:, e:256:2] for e in range(2)] + [vec_in[:, s : s + 128] for s in range(0, 384, 128)]
-            for i, v in enumerate(rows):
-                nc.tensor.transpose(tpv[:, 128 * i : 128 * i + 128], v, ident_b[:])
+            for i in range(6):
+                s = 256 * (i // 2) + i % 2
+                nc.tensor.transpose(tpv[:, 128 * i : 128 * i + 128], vec_in[:, s : min(s + 256, E) : 2], ident_b[:])
             nc.vector.tensor_copy(
-                out=vec_f[:].rearrange("p (i r) -> p i r", i=5),
-                in_=tpv[:, 0:640].rearrange("p (i r) -> p i r", i=5)[:, :, 0:8],
+                out=vec_f[:].rearrange("p (i r) -> p i r", i=6),
+                in_=tpv[:, 0:768].rearrange("p (i r) -> p i r", i=6)[:, :, 0:8],
             )
 
-        def col(i):
+        def col(j, e, row):
+            i = 8 * (2 * j + e) + row
             return vec_f[:, i : i + 1]
-
-        def col_w(row, n, e):
-            blk = 2 * (n - 5) + e
-            return col(8 * (2 + blk % 3) + row + blk // 3)
 
         hbf = [keep.tile([P, 1024], BF16, name="hbf%d" % g) for g in range(2)]
         grp_h = [keep.tile([P, 1024], BF16, name="grp_h%d" % g, align_bytes=64) for g in range(2)]
@@ -225,7 +224,7 @@ def tile_metalinearheadml_pb_kernel(tc, r, psi_w1, psi_b1, w_dw, b_dw, w_gate, b
             t = 2 * u + e
             dst = hbf[g2][:, 256 * t : 256 * t + 256]
             src = accs[n][u][:, 256 * u : 256 * u + 256]
-            bias = col(8 * e + 2 * g2 + u)
+            bias = col(u, e, g2)
             if on_vector:
                 nc.vector.tensor_scalar(out=dst, in0=src, scalar1=bias, scalar2=0.0, op0=ALU.add, op1=ALU.max)
             else:
@@ -241,7 +240,6 @@ def tile_metalinearheadml_pb_kernel(tc, r, psi_w1, psi_b1, w_dw, b_dw, w_gate, b
             nc.vector.quantize_mx(out=codes_h[g2][:].bitcast(FP8X4), scales=planes_h[g2][:], in_=grp_h[g2][:])
 
         out_sb = [keep.tile([P, 512], F32, name="out_sb%d" % j) for j in range(3)]
-        out_sb_e = keep.tile([P, 256], F32, name="out_sb_e")
         out_dram = out.rearrange("(a c) x -> c a x", a=2)
         accg, accd, gates, xs, fins = {}, {}, {}, {}, {}
 
@@ -270,16 +268,16 @@ def tile_metalinearheadml_pb_kernel(tc, r, psi_w1, psi_b1, w_dw, b_dw, w_gate, b
                 gates[n] = stage.tile([P, 512], F32, name="gate", tag="gate")
                 xs[n] = stage.tile([P, 512], F32, name="x", tag="x")
             cs = slice(256 * e, 256 * e + 256)
-            nc.scalar.activation(out=gates[n][:, cs], in_=accg[n][:, cs], func=ACT.Sigmoid, bias=col_w(6, n, e))
+            nc.scalar.activation(out=gates[n][:, cs], in_=accg[n][:, cs], func=ACT.Sigmoid, bias=col(n - 5, e, 3))
 
         def stt(n, e):
             cs = slice(256 * e, 256 * e + 256)
             nc.vector.scalar_tensor_tensor(
-                out=xs[n][:, cs], in0=accd[n][:, cs], scalar=col_w(4, n, e), in1=gates[n][:, cs], op0=ALU.add, op1=ALU.mult
+                out=xs[n][:, cs], in0=accd[n][:, cs], scalar=col(n - 5, e, 2), in1=gates[n][:, cs], op0=ALU.add, op1=ALU.mult
             )
 
         def back(n, e):
-            if e == 0 or n == 7:
+            if e == 0:
                 fins[(n, e)] = ps_pool.tile([P, 512], F32, name="fin", tag="ps")
             else:
                 fins[(n, e)] = fins[(n, 0)]
@@ -288,22 +286,16 @@ def tile_metalinearheadml_pb_kernel(tc, r, psi_w1, psi_b1, w_dw, b_dw, w_gate, b
                     fins[(n, e)][:, 256 * a + 128 * e : 256 * a + 128 * e + 128], xs[n][:, 256 * e + 128 * a : 256 * e + 128 * a + 128], ident_f[:]
                 )
 
-        def fin(n, e=None):
+        def fin(n):
             j = n - 5
-            lo, hi = (0, 256) if e is None else (128 * e, 128 * e + 128)
-            xc = slice(256 * j + lo, 256 * j + hi)
-            ov = out_sb[j][:].rearrange("c (a x) -> c a x", a=2)[:, :, lo:hi]
-            if e == 1:
-                ov = out_sb_e[:].rearrange("c (a x) -> c a x", a=2)
-            elif e == 0:
-                ov = out_sb[j][:, 0:256].rearrange("c (a x) -> c a x", a=2)
+            xc = slice(256 * j, 256 * j + 256)
             nc.vector.tensor_tensor(
-                out=ov,
-                in0=fins[(n, 0 if e is None else e)][:].rearrange("c (a x) -> c a x", a=2)[:, :, lo:hi],
-                in1=w0_b[:, xc].unsqueeze(1).to_broadcast([P, 2, hi - lo]),
+                out=out_sb[j][:].rearrange("c (a p e) -> c a p e", a=2, e=2),
+                in0=fins[(n, 0)][:].rearrange("c (a e p) -> c a p e", a=2, e=2),
+                in1=w0_b[:, xc].rearrange("c (p e) -> c p e", e=2).unsqueeze(1).to_broadcast([P, 2, 128, 2]),
                 op=ALU.add,
             )
-            nc.sync.dma_start(out=out_dram[:, :, xc], in_=ov)
+            nc.sync.dma_start(out=out_dram[:, :, xc], in_=out_sb[j][:].rearrange("c (a x) -> c a x", a=2))
 
         tr(0, 0)
         tr(0, 1)
@@ -313,29 +305,28 @@ def tile_metalinearheadml_pb_kernel(tc, r, psi_w1, psi_b1, w_dw, b_dw, w_gate, b
         tr(1, 1)
         qh(0, 0)
         qh(0, 1)
-        vec_prep()
         evh(1, 0)
         evh(1, 1)
         tr(2, 0)
         tr(2, 1)
         qh(1, 0)
         qh(1, 1)
-        evh(2, 0)
-        evh(2, 1)
-        tr(3, 0)
         mmh(1, 0)
         mmh(1, 1)
-        tr(3, 1)
+        evh(2, 0)
+        evh(2, 1)
+        vec_order()
+        tr(3, 0)
         qh(2, 0)
         qh(2, 1)
+        vec_prep()
+        tr(3, 1)
         evh(3, 0)
         evh(3, 1)
-        relu(1, 0)
-        relu(1, 1)
         mmh(2, 0)
         mmh(2, 1)
-        reorder(4, 0)
-        reorder(4, 1)
+        relu(1, 0)
+        relu(1, 1)
         tr(4, 0)
         tr(4, 1)
         qh(3, 0)
@@ -367,7 +358,7 @@ def tile_metalinearheadml_pb_kernel(tc, r, psi_w1, psi_b1, w_dw, b_dw, w_gate, b
         reorder(7, 0)
         reorder(7, 1)
         relu(4, 0)
-        relu(4, 1, True)
+        relu(4, 1)
         qh(5, 0)
         regroup(1)
         qh(5, 1)
@@ -381,21 +372,22 @@ def tile_metalinearheadml_pb_kernel(tc, r, psi_w1, psi_b1, w_dw, b_dw, w_gate, b
         trs(7, 3)
         qh(6, 0)
         qh(6, 1)
+
         ev(7, 0)
         ev(7, 1)
-        sig(5, 0)
-        sig(5, 1)
         ev(7, 2)
         evs(7, 3)
         qh(7, 0)
-        stt(5, 0)
-        stt(5, 1)
+        sig(5, 0)
+        sig(5, 1)
         mmo(6, 0)
         mmo(6, 1)
         sig(6, 0)
         sig(6, 1)
         q(7, 2, 3)
         q(7, 3, 4)
+        stt(5, 0)
+        stt(5, 1)
         mmo(7, 0)
         mmo1(7, 1, 0)
         mmo1(7, 1, 1)
@@ -413,5 +405,4 @@ def tile_metalinearheadml_pb_kernel(tc, r, psi_w1, psi_b1, w_dw, b_dw, w_gate, b
         fin(6)
         back(7, 0)
         back(7, 1)
-        fin(7, 0)
-        fin(7, 1)
+        fin(7)

@@ -15,9 +15,7 @@ P = 128
 C, R, HD, E = 256, 2048, 1024, 768
 FLOPS = 2 * C * R * HD + 2 * 2 * C * HD * E
 
-V_BANKS = {0: (1, 3), 1: (3,), 2: (3,), 3: (3,), 4: (), 5: (), 6: (), 7: ()}
-BY_K = (1, 2)
-REORDER = {(5, 0): "V", (5, 1): "V", (6, 0): "V", (6, 1): "V", (7, 0): "V", (7, 1): "V"}
+V_BANKS = {0: (1, 3), 1: (3,), 2: (3,), 3: (3,), 4: (3,), 5: (3,), 6: (3,), 7: ()}
 
 
 def tile_metalinearheadml_pb_kernel(tc, r, psi_w1, psi_b1, w_dw, b_dw, w_gate, b_gate, W0, out):
@@ -40,10 +38,6 @@ def tile_metalinearheadml_pb_kernel(tc, r, psi_w1, psi_b1, w_dw, b_dw, w_gate, b
         nc.scalar.dma_start(out=vec_in[3:4, :], in_=b_gate.rearrange("(o w) -> o w", o=1))
         ident_f = keep.tile([P, P], F32, name="ident_f")
         make_identity(nc, ident_f[:])
-        perm_f = keep.tile([P, P], F32, name="perm_f")
-        nc.gpsimd.tensor_copy(
-            out=perm_f[:].rearrange("p (v b) -> p v b", v=2), in_=ident_f[:].rearrange("p (b v) -> p v b", v=2)
-        )
         ident_b = keep.tile([P, P], BF16, name="ident_b")
         make_identity(nc, ident_b[:])
 
@@ -55,22 +49,12 @@ def tile_metalinearheadml_pb_kernel(tc, r, psi_w1, psi_b1, w_dw, b_dw, w_gate, b
             for b in range(2):
                 r_sb.append([t[:].bitcast(F32)[:, 512 * a + 256 * b : 512 * a + 256 * b + 256] for a in range(2)])
         unit_sb = {}
-        psi_dram = psi_w1.rearrange("(g p i e) k -> g e p i k", g=2, i=2, e=2)
-        psi_sb = {}
+        psi_dram = psi_w1.rearrange("(g p u e) k -> g u e p k", g=2, u=2, e=2)
         for n in range(1, 5):
-            src = psi_dram[(n - 1) // 2, (n - 1) % 2]
             t = keep.tile([P, 2 * R], BF16, name="unit%d" % n)
-            for h in range(2):
-                if n in BY_K:
-                    half = t[:, R * h : R * h + R].rearrange("p (i k) -> p i k", i=2)
-                    nc.sync.dma_start(out=half, in_=src[:, :, 1024 * h : 1024 * h + 1024])
-                    for b in range(2):
-                        psi_sb[(n, 2 * h + b)] = [t[:].bitcast(F32)[:, 1024 * h + 512 * i + 256 * b : 1024 * h + 512 * i + 256 * b + 256] for i in range(2)]
-                else:
-                    nc.sync.dma_start(out=t[:, R * h : R * h + R], in_=src[:, h])
-            if n not in BY_K:
-                for b in range(4):
-                    psi_sb[(n, b)] = [t[:].bitcast(F32)[:, 1024 * i + 256 * b : 1024 * i + 256 * b + 256] for i in range(2)]
+            for e in range(2):
+                nc.sync.dma_start(out=t[:, R * e : R * e + R], in_=psi_dram[(n - 1) // 2, (n - 1) % 2, e])
+            unit_sb[n] = t
         gt_dram = w_gate.rearrange("(j p e) k -> j p (e k)", j=3, e=2)
         dw_dram = w_dw.rearrange("(j p e) k -> j p (e k)", j=3, e=2)
         for j in range(3):
@@ -85,33 +69,18 @@ def tile_metalinearheadml_pb_kernel(tc, r, psi_w1, psi_b1, w_dw, b_dw, w_gate, b
         planes = [keep.tile([P, 1024], U8, name="planes%d" % n, align_bytes=64) for n in range(8)]
         groups = {}
         banks = {}
-        re_sb = {}
-
-        def reorder(n, h):
-            if (n, h) not in REORDER:
-                return
-            if n not in re_sb:
-                re_sb[n] = keep.tile([P, 4096], BF16, name="re_sb%d" % n)
-            i = unit_sb[n][:, 2048 * h : 2048 * h + 2048].rearrange("p (b u x) -> p u b x", u=2, x=4)
-            o = re_sb[n][:, 2048 * h : 2048 * h + 2048].rearrange("p (u b x) -> p u b x", u=2, x=4)
-            if REORDER.get((n, h), "V") == "V":
-                nc.vector.tensor_copy(out=o, in_=i)
-            else:
-                nc.scalar.copy(out=o, in_=i)
 
         def slices_of(n, b):
             if n == 0:
                 return [r_sb[b][a][:, u:256:2] for u in range(2) for a in range(2)]
-            if n < 5:
-                return [psi_sb[(n, b)][i][:, u:256:2] for i in range(2) for u in range(2)]
-            src = re_sb[n][:].bitcast(F32)
-            starts = [1024 * (b % 2) + 512 * u + 256 * (b // 2) + 128 * g for g in range(2) for u in range(2)]
-            return [src[:, s : s + 128] for s in starts]
+            src = unit_sb[n][:].bitcast(F32)
+            base = 512 * b if n < 5 else 1024 * (b % 2) + 512 * (b // 2)
+            return [src[:, base + 256 * g + u : base + 256 * g + 256 : 2] for g in range(2) for u in range(2)]
 
         def trb(n, b):
             tp = ps_pool.tile([P, 512], F32, name="tp", tag="ps")
             for i, s in enumerate(slices_of(n, b)):
-                nc.tensor.transpose(tp[:, 128 * i : 128 * i + 128], s, perm_f[:] if 1 <= n <= 4 else ident_f[:])
+                nc.tensor.transpose(tp[:, 128 * i : 128 * i + 128], s, ident_f[:])
             banks[(n, b)] = tp
 
         def tr(n, h):
@@ -137,9 +106,6 @@ def tile_metalinearheadml_pb_kernel(tc, r, psi_w1, psi_b1, w_dw, b_dw, w_gate, b
             if n == 0:
                 dst = dst.rearrange("q (c u) -> q c u", u=2)
                 i = tp[:].rearrange("q (u c) -> q c u", u=2)
-            elif n < 5:
-                dst = dst.rearrange("q (v b x) -> q v b x", v=2, x=4)
-                i = tp[:].rearrange("q (x v b) -> q v b x", x=4, v=2)
             else:
                 dst = dst.rearrange("q (g m u) -> q g m u", g=2, u=2)
                 i = tp[:].rearrange("q (g u m) -> q g m u", g=2, u=2)
@@ -175,8 +141,8 @@ def tile_metalinearheadml_pb_kernel(tc, r, psi_w1, psi_b1, w_dw, b_dw, w_gate, b
 
         def vec_order():
             nc.vector.tensor_copy(
-                out=vec_in[0:2, 0:512].rearrange("p (u b x) -> p u b x", u=2, x=4),
-                in_=b1_raw[:].rearrange("p (b u x) -> p u b x", u=2, x=4),
+                out=vec_in[0:2, 0:512].rearrange("p (u b x) -> p u b x", u=2, x=2),
+                in_=b1_raw[:].rearrange("p (b u x) -> p u b x", u=2, x=2),
             )
 
         def vec_prep():
@@ -207,7 +173,7 @@ def tile_metalinearheadml_pb_kernel(tc, r, psi_w1, psi_b1, w_dw, b_dw, w_gate, b
             else:
                 accs[n][e] = accs[n][0]
             for g in range(4):
-                cols = slice((2 * g + e) * 128, (2 * g + e) * 128 + 128)
+                cols = slice((4 * e + g) * 128, (4 * e + g) * 128 + 128)
                 rc = slice(256 * g, 256 * g + 256)
                 nc.tensor.matmul_mx(
                     out=accs[n][e][:, 256 * e : 256 * e + 256],
@@ -219,11 +185,11 @@ def tile_metalinearheadml_pb_kernel(tc, r, psi_w1, psi_b1, w_dw, b_dw, w_gate, b
                     stop=(g == 3),
                 )
 
-        def relu(n, u, on_vector=False):
-            g2, e = (n - 1) // 2, (n - 1) % 2
+        def relu(n, e, on_vector=False):
+            g2, u = (n - 1) // 2, (n - 1) % 2
             t = 2 * u + e
             dst = hbf[g2][:, 256 * t : 256 * t + 256]
-            src = accs[n][u][:, 256 * u : 256 * u + 256]
+            src = accs[n][e][:, 256 * e : 256 * e + 256]
             bias = col(u, e, g2)
             if on_vector:
                 nc.vector.tensor_scalar(out=dst, in0=src, scalar1=bias, scalar2=0.0, op0=ALU.add, op1=ALU.max)
@@ -335,8 +301,6 @@ def tile_metalinearheadml_pb_kernel(tc, r, psi_w1, psi_b1, w_dw, b_dw, w_gate, b
         mmh(3, 1)
         relu(2, 0)
         relu(2, 1)
-        reorder(5, 0)
-        reorder(5, 1)
         evh(4, 0)
         evh(4, 1)
         tr(5, 0)
@@ -349,14 +313,10 @@ def tile_metalinearheadml_pb_kernel(tc, r, psi_w1, psi_b1, w_dw, b_dw, w_gate, b
         mmh(4, 1)
         relu(3, 0)
         relu(3, 1)
-        reorder(6, 0)
-        reorder(6, 1)
         evh(5, 0)
         evh(5, 1)
         tr(6, 0)
         tr(6, 1)
-        reorder(7, 0)
-        reorder(7, 1)
         relu(4, 0)
         relu(4, 1)
         qh(5, 0)
@@ -372,7 +332,6 @@ def tile_metalinearheadml_pb_kernel(tc, r, psi_w1, psi_b1, w_dw, b_dw, w_gate, b
         trs(7, 3)
         qh(6, 0)
         qh(6, 1)
-
         ev(7, 0)
         ev(7, 1)
         ev(7, 2)

@@ -15,7 +15,7 @@ P = 128
 C, R, HD, E = 256, 2048, 1024, 768
 FLOPS = 2 * C * R * HD + 2 * 2 * C * HD * E
 
-V_BANKS = {0: (1, 3), 1: (3,), 2: (3,), 3: (3,), 4: (3,), 5: (3,), 6: (3,), 7: ()}
+V_BANKS = {0: (1, 3), 1: (3,), 2: (3,), 3: (3,), 4: (3,), 5: (), 6: (), 7: (1,)}
 
 
 def tile_metalinearheadml_pb_kernel(tc, r, psi_w1, psi_b1, w_dw, b_dw, w_gate, b_gate, W0, out):
@@ -38,9 +38,6 @@ def tile_metalinearheadml_pb_kernel(tc, r, psi_w1, psi_b1, w_dw, b_dw, w_gate, b
         nc.scalar.dma_start(out=vec_in[3:4, :], in_=b_gate.rearrange("(o w) -> o w", o=1))
         ident_f = keep.tile([P, P], F32, name="ident_f")
         make_identity(nc, ident_f[:])
-        ident_b = keep.tile([P, P], BF16, name="ident_b")
-        make_identity(nc, ident_b[:])
-
         r_dram = r.rearrange("(a p) k -> p a k", a=2)
         r_sb = []
         for h in range(2):
@@ -137,6 +134,7 @@ def tile_metalinearheadml_pb_kernel(tc, r, psi_w1, psi_b1, w_dw, b_dw, w_gate, b
         def qh(n, h):
             q(n, 2 * h, 2 * h + 2)
 
+        vec_w = keep.tile([P, 24], F32, name="vec_w")
         vec_f = keep.tile([P, 48], F32, name="vec_f")
 
         def vec_order():
@@ -146,17 +144,20 @@ def tile_metalinearheadml_pb_kernel(tc, r, psi_w1, psi_b1, w_dw, b_dw, w_gate, b
             )
 
         def vec_prep():
-            tpv = ps_pool.tile([P, 1024], BF16, name="tpv", tag="ps")
-            for i in range(6):
-                s = 256 * (i // 2) + i % 2
-                nc.tensor.transpose(tpv[:, 128 * i : 128 * i + 128], vec_in[:, s : min(s + 256, E) : 2], ident_b[:])
+            tpv = ps_pool.tile([P, 512], F32, name="tpv", tag="ps")
+            words = vec_in[:].bitcast(F32)
+            for j in range(3):
+                nc.tensor.transpose(tpv[:, 128 * j : 128 * j + 128], words[:, 128 * j : 128 * j + 128], ident_f[:])
             nc.vector.tensor_copy(
-                out=vec_f[:].rearrange("p (i r) -> p i r", i=6),
-                in_=tpv[:, 0:768].rearrange("p (i r) -> p i r", i=6)[:, :, 0:8],
+                out=vec_w[:].rearrange("p (j r) -> p j r", j=3),
+                in_=tpv[:, 0:384].rearrange("p (j r) -> p j r", j=3)[:, :, 0:8],
             )
 
+        def vec_cast():
+            nc.vector.tensor_copy(out=vec_f[:], in_=vec_w[:].bitcast(BF16))
+
         def col(j, e, row):
-            i = 8 * (2 * j + e) + row
+            i = 2 * (8 * j + row) + e
             return vec_f[:, i : i + 1]
 
         hbf = [keep.tile([P, 1024], BF16, name="hbf%d" % g) for g in range(2)]
@@ -252,16 +253,19 @@ def tile_metalinearheadml_pb_kernel(tc, r, psi_w1, psi_b1, w_dw, b_dw, w_gate, b
                     fins[(n, e)][:, 256 * a + 128 * e : 256 * a + 128 * e + 128], xs[n][:, 256 * e + 128 * a : 256 * e + 128 * a + 128], ident_f[:]
                 )
 
-        def fin(n):
+        def fin(n, parts=1):
             j = n - 5
             xc = slice(256 * j, 256 * j + 256)
-            nc.vector.tensor_tensor(
-                out=out_sb[j][:].rearrange("c (a p e) -> c a p e", a=2, e=2),
-                in0=fins[(n, 0)][:].rearrange("c (a e p) -> c a p e", a=2, e=2),
-                in1=w0_b[:, xc].rearrange("c (p e) -> c p e", e=2).unsqueeze(1).to_broadcast([P, 2, 128, 2]),
-                op=ALU.add,
-            )
-            nc.sync.dma_start(out=out_dram[:, :, xc], in_=out_sb[j][:].rearrange("c (a x) -> c a x", a=2))
+            for k in range(parts):
+                w = 2 // parts
+                c = slice(256 * w * k, 256 * w * k + 256 * w)
+                nc.vector.tensor_tensor(
+                    out=out_sb[j][:, c].rearrange("c (a p e) -> c a p e", a=w, e=2),
+                    in0=fins[(n, 0)][:, c].rearrange("c (a e p) -> c a p e", a=w, e=2),
+                    in1=w0_b[:, xc].rearrange("c (p e) -> c p e", e=2).unsqueeze(1).to_broadcast([P, w, 128, 2]),
+                    op=ALU.add,
+                )
+                nc.sync.dma_start(out=out_dram[:, w * k : w * k + w, xc], in_=out_sb[j][:, c].rearrange("c (a x) -> c a x", a=w))
 
         tr(0, 0)
         tr(0, 1)
@@ -287,51 +291,53 @@ def tile_metalinearheadml_pb_kernel(tc, r, psi_w1, psi_b1, w_dw, b_dw, w_gate, b
         qh(2, 1)
         vec_prep()
         tr(3, 1)
+        vec_cast()
+        mmh(2, 0)
         evh(3, 0)
         evh(3, 1)
-        mmh(2, 0)
-        mmh(2, 1)
         relu(1, 0)
         relu(1, 1)
         tr(4, 0)
         tr(4, 1)
         qh(3, 0)
         qh(3, 1)
+        mmh(2, 1)
         mmh(3, 0)
-        mmh(3, 1)
-        relu(2, 0)
-        relu(2, 1)
         evh(4, 0)
         evh(4, 1)
+        relu(2, 0)
+        relu(2, 1)
         tr(5, 0)
         tr(5, 1)
-        regroup(0)
         qh(4, 0)
-        quant_hidden(0)
         qh(4, 1)
+        mmh(3, 1)
         mmh(4, 0)
-        mmh(4, 1)
-        relu(3, 0)
-        relu(3, 1)
+        regroup(0)
         evh(5, 0)
         evh(5, 1)
+        relu(3, 0)
+        relu(3, 1)
         tr(6, 0)
         tr(6, 1)
-        relu(4, 0)
-        relu(4, 1)
+        quant_hidden(0)
         qh(5, 0)
-        regroup(1)
+        mmh(4, 1)
         qh(5, 1)
-        quant_hidden(1)
+        relu(4, 0)
         evh(6, 0)
+        relu(4, 1)
+        qh(6, 0)
+        regroup(1)
+        quant_hidden(1)
         evh(6, 1)
         tr(7, 0)
-        mmo(5, 0)
-        mmo(5, 1)
         trb(7, 2)
         trs(7, 3)
-        qh(6, 0)
+        mmo(5, 0)
+        mmo(5, 1)
         qh(6, 1)
+
         ev(7, 0)
         ev(7, 1)
         ev(7, 2)
@@ -364,4 +370,4 @@ def tile_metalinearheadml_pb_kernel(tc, r, psi_w1, psi_b1, w_dw, b_dw, w_gate, b
         fin(6)
         back(7, 0)
         back(7, 1)
-        fin(7)
+        fin(7, 2)

from contextlib import ExitStack

import concourse.mybir as mybir
from concourse.masks import make_identity

F32 = mybir.dt.float32
BF16 = mybir.dt.bfloat16
U32 = mybir.dt.uint32
U8 = mybir.dt.uint8
FP8X4 = mybir.dt.float8_e4m3fn_x4
ACT = mybir.ActivationFunctionType
ALU = mybir.AluOpType

P = 128
C, R, HD, E = 256, 2048, 1024, 768
FLOPS = 2 * C * R * HD + 2 * 2 * C * HD * E

V_BANKS = {0: (1, 3), 1: (3,), 2: (3,), 3: (3,), 4: (3,), 5: (), 6: (), 7: (1,)}


def tile_metalinearheadml_pb_kernel(tc, r, psi_w1, psi_b1, w_dw, b_dw, w_gate, b_gate, W0, out):
    nc = tc.nc
    with ExitStack() as ctx:
        keep = ctx.enter_context(tc.tile_pool(name="keep", bufs=1))
        stage = ctx.enter_context(tc.tile_pool(name="stage", bufs=3))
        ps_pool = ctx.enter_context(tc.psum_pool(name="ps_pool", bufs=8))
        ctx.enter_context(tc.manual_schedule())

        warm = keep.tile([P, 1], F32, name="warm")
        nc.vector.memset(warm[:], 0.0)
        warm2 = keep.tile([P, 1], F32, name="warm2")
        nc.scalar.activation(out=warm2[:], in_=warm[:], func=ACT.Sigmoid)
        vec_in = keep.tile([P, E], BF16, name="vec_in")
        nc.vector.memset(vec_in[:], 0.0)
        b1_raw = keep.tile([2, 512], BF16, name="b1_raw")
        nc.scalar.dma_start(out=b1_raw[:], in_=psi_b1.rearrange("(a w) -> a w", a=2))
        nc.scalar.dma_start(out=vec_in[2:3, :], in_=b_dw.rearrange("(o w) -> o w", o=1))
        nc.scalar.dma_start(out=vec_in[3:4, :], in_=b_gate.rearrange("(o w) -> o w", o=1))
        ident_f = keep.tile([P, P], F32, name="ident_f")
        make_identity(nc, ident_f[:])
        r_dram = r.rearrange("(a p) k -> p a k", a=2)
        r_sb = []
        for h in range(2):
            t = keep.tile([P, R], BF16, name="r_sb%d" % h)
            nc.sync.dma_start(out=t[:].rearrange("p (a k) -> p a k", a=2), in_=r_dram[:, :, 1024 * h : 1024 * h + 1024])
            for b in range(2):
                r_sb.append([t[:].bitcast(F32)[:, 512 * a + 256 * b : 512 * a + 256 * b + 256] for a in range(2)])
        unit_sb = {}
        psi_dram = psi_w1.rearrange("(g p u e) k -> g u e p k", g=2, u=2, e=2)
        for n in range(1, 5):
            t = keep.tile([P, 2 * R], BF16, name="unit%d" % n)
            for e in range(2):
                nc.sync.dma_start(out=t[:, R * e : R * e + R], in_=psi_dram[(n - 1) // 2, (n - 1) % 2, e])
            unit_sb[n] = t
        gt_dram = w_gate.rearrange("(j p e) k -> j p (e k)", j=3, e=2)
        dw_dram = w_dw.rearrange("(j p e) k -> j p (e k)", j=3, e=2)
        for j in range(3):
            t = keep.tile([P, 2 * R], BF16, name="unit%d" % (5 + j))
            nc.sync.dma_start(out=t[:, 0:R], in_=gt_dram[j])
            nc.sync.dma_start(out=t[:, R : 2 * R], in_=dw_dram[j])
            unit_sb[5 + j] = t
        w0_b = keep.tile([P, E], BF16, name="w0_b")
        nc.sync.dma_start(out=w0_b[:], in_=W0.partition_broadcast(P))

        codes = [keep.tile([P, 1024], U32, name="codes%d" % n, align_bytes=64) for n in range(8)]
        planes = [keep.tile([P, 1024], U8, name="planes%d" % n, align_bytes=64) for n in range(8)]
        groups = {}
        banks = {}

        def slices_of(n, b):
            if n == 0:
                return [r_sb[b][a][:, u:256:2] for u in range(2) for a in range(2)]
            src = unit_sb[n][:].bitcast(F32)
            base = 512 * b if n < 5 else 1024 * (b % 2) + 512 * (b // 2)
            return [src[:, base + 256 * g + u : base + 256 * g + 256 : 2] for g in range(2) for u in range(2)]

        def trb(n, b):
            tp = ps_pool.tile([P, 512], F32, name="tp", tag="ps")
            for i, s in enumerate(slices_of(n, b)):
                nc.tensor.transpose(tp[:, 128 * i : 128 * i + 128], s, ident_f[:])
            banks[(n, b)] = tp

        def tr(n, h):
            trb(n, 2 * h)
            trb(n, 2 * h + 1)

        def trs(n, b):
            banks[(n, b)] = []
            for g in range(2):
                tp = ps_pool.tile([P, 512], F32, name="tp", tag="ps")
                for u in range(2):
                    nc.tensor.transpose(tp[:, 128 * u : 128 * u + 128], slices_of(n, b)[2 * g + u], ident_f[:])
                banks[(n, b)].append(tp)

        def group(n):
            if n not in groups:
                groups[n] = stage.tile([P, 4096], BF16, name="grp", tag="grp", align_bytes=64)
            return groups[n][:].bitcast(F32)

        def ev(n, b):
            tp = banks[(n, b)]
            dst = group(n)[:, 512 * b : 512 * b + 512]
            if n == 0:
                dst = dst.rearrange("q (c u) -> q c u", u=2)
                i = tp[:].rearrange("q (u c) -> q c u", u=2)
            else:
                dst = dst.rearrange("q (g m u) -> q g m u", g=2, u=2)
                i = tp[:].rearrange("q (g u m) -> q g m u", g=2, u=2)
            if b in V_BANKS[n]:
                nc.vector.tensor_copy(out=dst, in_=i)
            else:
                nc.scalar.copy(out=dst, in_=i)

        def evs(n, b):
            for g in range(2):
                dst = group(n)[:, 512 * b + 256 * g : 512 * b + 256 * g + 256].rearrange("q (m u) -> q m u", u=2)
                i = banks[(n, b)][g][:, 0:256].rearrange("q (u m) -> q m u", u=2)
                if g:
                    nc.vector.tensor_copy(out=dst, in_=i)
                else:
                    nc.scalar.copy(out=dst, in_=i)

        def evh(n, h):
            ev(n, 2 * h)
            ev(n, 2 * h + 1)

        def q(n, lo, hi):
            nc.vector.quantize_mx(
                out=codes[n][:, 256 * lo : 256 * hi].bitcast(FP8X4),
                scales=planes[n][:, 256 * lo : 256 * hi],
                in_=groups[n][:, 1024 * lo : 1024 * hi],
            )

        def qh(n, h):
            q(n, 2 * h, 2 * h + 2)

        vec_w = keep.tile([P, 24], F32, name="vec_w")
        vec_f = keep.tile([P, 48], F32, name="vec_f")

        def vec_order():
            nc.vector.tensor_copy(
                out=vec_in[0:2, 0:512].rearrange("p (u b x) -> p u b x", u=2, x=2),
                in_=b1_raw[:].rearrange("p (b u x) -> p u b x", u=2, x=2),
            )

        def vec_prep():
            tpv = ps_pool.tile([P, 512], F32, name="tpv", tag="ps")
            words = vec_in[:].bitcast(F32)
            for j in range(3):
                nc.tensor.transpose(tpv[:, 128 * j : 128 * j + 128], words[:, 128 * j : 128 * j + 128], ident_f[:])
            nc.vector.tensor_copy(
                out=vec_w[:].rearrange("p (j r) -> p j r", j=3),
                in_=tpv[:, 0:384].rearrange("p (j r) -> p j r", j=3)[:, :, 0:8],
            )

        def vec_cast():
            nc.vector.tensor_copy(out=vec_f[:], in_=vec_w[:].bitcast(BF16))

        def col(j, e, row):
            i = 2 * (8 * j + row) + e
            return vec_f[:, i : i + 1]

        hbf = [keep.tile([P, 1024], BF16, name="hbf%d" % g) for g in range(2)]
        grp_h = [keep.tile([P, 1024], BF16, name="grp_h%d" % g, align_bytes=64) for g in range(2)]
        codes_h = [keep.tile([P, 256], U32, name="codes_h%d" % g, align_bytes=64) for g in range(2)]
        planes_h = [keep.tile([P, 256], U8, name="planes_h%d" % g, align_bytes=64) for g in range(2)]
        accs = {}

        def mmh(n, e):
            if n not in accs:
                accs[n] = {}
            if e == 0 or n == 4:
                accs[n][e] = ps_pool.tile([P, 512], F32, name="acc1", tag="ps")
            else:
                accs[n][e] = accs[n][0]
            for g in range(4):
                cols = slice((4 * e + g) * 128, (4 * e + g) * 128 + 128)
                rc = slice(256 * g, 256 * g + 256)
                nc.tensor.matmul_mx(
                    out=accs[n][e][:, 256 * e : 256 * e + 256],
                    lhsT=codes[n][:, cols].bitcast(FP8X4),
                    lhsT_scale=planes[n][:, cols],
                    rhs=codes[0][:, rc].bitcast(FP8X4),
                    rhs_scale=planes[0][:, rc],
                    start=(g == 0),
                    stop=(g == 3),
                )

        def relu(n, e, on_vector=False):
            g2, u = (n - 1) // 2, (n - 1) % 2
            t = 2 * u + e
            dst = hbf[g2][:, 256 * t : 256 * t + 256]
            src = accs[n][e][:, 256 * e : 256 * e + 256]
            bias = col(u, e, g2)
            if on_vector:
                nc.vector.tensor_scalar(out=dst, in0=src, scalar1=bias, scalar2=0.0, op0=ALU.add, op1=ALU.max)
            else:
                nc.scalar.activation(out=dst, in_=src, func=ACT.Relu, bias=bias)

        def regroup(g2):
            nc.vector.tensor_copy(
                out=grp_h[g2][:].rearrange("p (c i t) -> p c t i", i=4, t=4),
                in_=hbf[g2][:].rearrange("p (t c i) -> p c t i", t=4, i=4),
            )

        def quant_hidden(g2):
            nc.vector.quantize_mx(out=codes_h[g2][:].bitcast(FP8X4), scales=planes_h[g2][:], in_=grp_h[g2][:])

        out_sb = [keep.tile([P, 512], F32, name="out_sb%d" % j) for j in range(3)]
        out_dram = out.rearrange("(a c) x -> c a x", a=2)
        accg, accd, gates, xs, fins = {}, {}, {}, {}, {}

        def mmo1(n, e, m):
            store = (accg, accd)[m]
            if e == 0:
                store[n] = ps_pool.tile([P, 512], F32, name="acc2", tag="ps")
            for g2 in range(2):
                cols = slice(((2 * e + m) * 2 + g2) * 128, ((2 * e + m) * 2 + g2) * 128 + 128)
                nc.tensor.matmul_mx(
                    out=store[n][:, 256 * e : 256 * e + 256],
                    lhsT=codes[n][:, cols].bitcast(FP8X4),
                    lhsT_scale=planes[n][:, cols],
                    rhs=codes_h[g2][:].bitcast(FP8X4),
                    rhs_scale=planes_h[g2][:],
                    start=(g2 == 0),
                    stop=(g2 == 1),
                )

        def mmo(n, e):
            mmo1(n, e, 0)
            mmo1(n, e, 1)

        def sig(n, e):
            if e == 0:
                gates[n] = stage.tile([P, 512], F32, name="gate", tag="gate")
                xs[n] = stage.tile([P, 512], F32, name="x", tag="x")
            cs = slice(256 * e, 256 * e + 256)
            nc.scalar.activation(out=gates[n][:, cs], in_=accg[n][:, cs], func=ACT.Sigmoid, bias=col(n - 5, e, 3))

        def stt(n, e):
            cs = slice(256 * e, 256 * e + 256)
            nc.vector.scalar_tensor_tensor(
                out=xs[n][:, cs], in0=accd[n][:, cs], scalar=col(n - 5, e, 2), in1=gates[n][:, cs], op0=ALU.add, op1=ALU.mult
            )

        def back(n, e):
            if e == 0:
                fins[(n, e)] = ps_pool.tile([P, 512], F32, name="fin", tag="ps")
            else:
                fins[(n, e)] = fins[(n, 0)]
            for a in range(2):
                nc.tensor.transpose(
                    fins[(n, e)][:, 256 * a + 128 * e : 256 * a + 128 * e + 128], xs[n][:, 256 * e + 128 * a : 256 * e + 128 * a + 128], ident_f[:]
                )

        def fin(n, parts=1):
            j = n - 5
            xc = slice(256 * j, 256 * j + 256)
            for k in range(parts):
                w = 2 // parts
                c = slice(256 * w * k, 256 * w * k + 256 * w)
                nc.vector.tensor_tensor(
                    out=out_sb[j][:, c].rearrange("c (a p e) -> c a p e", a=w, e=2),
                    in0=fins[(n, 0)][:, c].rearrange("c (a e p) -> c a p e", a=w, e=2),
                    in1=w0_b[:, xc].rearrange("c (p e) -> c p e", e=2).unsqueeze(1).to_broadcast([P, w, 128, 2]),
                    op=ALU.add,
                )
                nc.sync.dma_start(out=out_dram[:, w * k : w * k + w, xc], in_=out_sb[j][:, c].rearrange("c (a x) -> c a x", a=w))

        tr(0, 0)
        tr(0, 1)
        evh(0, 0)
        evh(0, 1)
        tr(1, 0)
        tr(1, 1)
        qh(0, 0)
        qh(0, 1)
        evh(1, 0)
        evh(1, 1)
        tr(2, 0)
        tr(2, 1)
        qh(1, 0)
        qh(1, 1)
        mmh(1, 0)
        mmh(1, 1)
        evh(2, 0)
        evh(2, 1)
        vec_order()
        tr(3, 0)
        qh(2, 0)
        qh(2, 1)
        vec_prep()
        tr(3, 1)
        vec_cast()
        mmh(2, 0)
        evh(3, 0)
        evh(3, 1)
        relu(1, 0)
        relu(1, 1)
        tr(4, 0)
        tr(4, 1)
        qh(3, 0)
        qh(3, 1)
        mmh(2, 1)
        mmh(3, 0)
        evh(4, 0)
        evh(4, 1)
        relu(2, 0)
        relu(2, 1)
        tr(5, 0)
        tr(5, 1)
        qh(4, 0)
        qh(4, 1)
        mmh(3, 1)
        mmh(4, 0)
        regroup(0)
        evh(5, 0)
        evh(5, 1)
        relu(3, 0)
        relu(3, 1)
        tr(6, 0)
        tr(6, 1)
        quant_hidden(0)
        qh(5, 0)
        mmh(4, 1)
        qh(5, 1)
        relu(4, 0)
        evh(6, 0)
        relu(4, 1)
        qh(6, 0)
        regroup(1)
        quant_hidden(1)
        evh(6, 1)
        tr(7, 0)
        trb(7, 2)
        trs(7, 3)
        mmo(5, 0)
        mmo(5, 1)
        qh(6, 1)

        ev(7, 0)
        ev(7, 1)
        ev(7, 2)
        evs(7, 3)
        qh(7, 0)
        sig(5, 0)
        sig(5, 1)
        mmo(6, 0)
        mmo(6, 1)
        sig(6, 0)
        sig(6, 1)
        q(7, 2, 3)
        q(7, 3, 4)
        stt(5, 0)
        stt(5, 1)
        mmo(7, 0)
        mmo1(7, 1, 0)
        mmo1(7, 1, 1)
        stt(6, 0)
        stt(6, 1)
        back(5, 0)
        back(5, 1)
        sig(7, 0)
        stt(7, 0)
        fin(5)
        back(6, 0)
        back(6, 1)
        sig(7, 1)
        stt(7, 1)
        fin(6)
        back(7, 0)
        back(7, 1)
        fin(7, 2)
